import numpy as np
import ml_dtypes


def mxq(x, axis, fmt="e4m3"):
    dtype, down = {"e4m3": (ml_dtypes.float8_e4m3fn, 7), "e5m2": (ml_dtypes.float8_e5m2, 14)}[fmt]
    v = np.moveaxis(np.asarray(x, np.float32).astype(ml_dtypes.bfloat16).astype(np.float64), axis, -1)
    blocks = v.reshape(v.shape[:-1] + (-1, 32))
    amax = np.abs(blocks).max(-1, keepdims=True)
    byte = np.maximum(np.where(amax > 0, np.frexp(amax)[1] - 1 + 127, 0) - down, 1)
    scale = np.exp2(byte - 127.0)
    codes = (blocks / scale).astype(np.float32).astype(dtype).astype(np.float64)
    return np.moveaxis((codes * scale).reshape(v.shape), -1, axis)


WIDE = False


def mx_kscale(k):
    if not WIDE:
        return np.ones(k)
    levels = np.array([10, -10, 5, -5, 0])
    a = np.random.permutation(np.resize(levels, k // 512 * 4)).reshape(k // 512, 4)
    idx = np.arange(k)
    return np.exp2(a[idx // 512, idx % 128 // 32])


BF16 = ml_dtypes.bfloat16


def bf(x):
    return np.asarray(x, np.float32).astype(BF16)


def f64(x):
    return np.asarray(x).astype(np.float64)


B, S, H, R = 4, 384, 1024, 3
N = S // R


def setup_inputs():
    t = mx_kscale(H)
    return {"h": bf(np.random.standard_normal((B, N, R, H))),
            "s2t_W1_w": bf(np.random.standard_normal((H, H)) / np.sqrt(H) * t[:, None]),
            "s2t_W1_b": bf(np.random.standard_normal(H) * 0.3 * t),
            "s2t_W_w": bf(np.random.standard_normal((H, H)) * 2.0 / np.sqrt(H) / t[None, :])}


def reference(h, s2t_W1_w, s2t_W1_b, s2t_W_w):
    hf = f64(h)
    rows = hf.reshape(B * N * R, H)
    f = np.maximum((mxq(rows, 1, "e4m3") @ mxq(f64(s2t_W1_w), 1, "e4m3").T) + f64(s2t_W1_b), 0.0)
    z = (mxq(f, 1, "e4m3") @ mxq(f64(s2t_W_w), 1, "e4m3").T).reshape(B, N, R, H)
    e = np.exp(z - z.max(-2, keepdims=True))
    p = e / e.sum(-2, keepdims=True)
    return (p * hf).sum(-2)

@@ -1,0 +1,360 @@
+from contextlib import ExitStack
+
+import concourse.mybir as mybir
+from concourse.masks import make_identity
+
+F32 = mybir.dt.float32
+BF16 = mybir.dt.bfloat16
+U32 = mybir.dt.uint32
+U8 = mybir.dt.uint8
+FP8X4 = mybir.dt.float8_e4m3fn_x4
+ACT = mybir.ActivationFunctionType
+ALU = mybir.AluOpType
+
+P = 128
+BATCHES = 4
+TOKENS = 3
+H = 1024
+PACK = 4
+PASSES = H // (P * PACK)
+PLANES = 2
+PIECE = 2 * P
+WEIGHT_PIECES = H // PIECE
+ROW_TILES = H // P
+BANK = 512
+HALVES = H // BANK
+RUN = 4
+LAG = 2
+
+FLOPS = 2 * 2 * BATCHES * P * TOKENS * H * H
+
+
+def tile_blocksa_pa_kernel(tc, h, s2t_W1_w, s2t_W1_b, s2t_W_w, out):
+    nc = tc.nc
+    h_flat = h.rearrange("b n j k -> (b n) (j k)")
+    out_flat = out.rearrange("b n c -> (b n) c")
+
+    with ExitStack() as stack:
+        consts = stack.enter_context(tc.tile_pool(name="consts", bufs=1))
+        keep = stack.enter_context(tc.tile_pool(name="keep", bufs=1))
+        raw = stack.enter_context(tc.tile_pool(name="raw", bufs=4))
+        stage = stack.enter_context(tc.tile_pool(name="stage", bufs=3))
+        hidden = stack.enter_context(tc.tile_pool(name="hidden", bufs=2))
+        work = stack.enter_context(tc.tile_pool(name="work", bufs=2))
+        psum = stack.enter_context(tc.psum_pool(name="psum", bufs=6))
+        psum_gap = stack.enter_context(tc.psum_pool(name="psum_gap", bufs=2))
+        stack.enter_context(tc.manual_schedule())
+
+        bias_rows = consts.tile([P, 2 * P], BF16)
+        nc.vector.memset(bias_rows[:], 0.0)
+        nc.sync.dma_start(
+            out=bias_rows[0:WEIGHT_PIECES, :],
+            in_=s2t_W1_b.rearrange("(r c) -> r c", r=WEIGHT_PIECES),
+        )
+        bias = consts.tile([P, ROW_TILES], F32)
+        half_col = consts.tile([P, 1], F32)
+        nc.vector.memset(half_col[:], 0.5)
+
+        ident = consts.tile([P, P], F32)
+        make_identity(nc, ident[:])
+        half_plus = consts.tile([P, P], BF16)
+        nc.vector.tensor_scalar_mul(out=half_plus[:], in0=ident[:], scalar1=0.5)
+        half_minus = consts.tile([P, P], BF16)
+        nc.vector.tensor_scalar_mul(out=half_minus[:], in0=ident[:], scalar1=-0.5)
+
+        def spread_bias():
+            bias_bank = psum.tile([P, BANK], F32, tag="bank")
+            nc.tensor.transpose(bias_bank[:, 0:P], bias_rows[:].bitcast(F32), ident[:])
+            bias_pairs = consts.tile([P, WEIGHT_PIECES], F32)
+            nc.vector.tensor_copy(out=bias_pairs[:], in_=bias_bank[:, 0:WEIGHT_PIECES])
+            nc.vector.tensor_copy(out=bias[:], in_=bias_pairs[:].bitcast(BF16))
+
+        warm = consts.tile([P, 1], F32)
+        nc.scalar.activation(out=warm[:], in_=half_col[:], func=ACT.Tanh)
+
+        h_rows = []
+        for b in range(BATCHES):
+            h_rows.append(keep.tile([P, TOKENS, H], BF16, name="h_rows%d" % b))
+
+        def load_tokens(b, first, last):
+            nc.sync.dma_start(
+                out=h_rows[b][:, first:last, :].rearrange("n j k -> n (j k)"),
+                in_=h_flat[b * P : (b + 1) * P, first * H : last * H],
+            )
+
+        load_tokens(0, 0, 2)
+
+        w1_raw = []
+        for r in range(WEIGHT_PIECES):
+            rows = raw.tile([P, 2, H], BF16, tag="raw", name="w1_raw%d" % r)
+            nc.sync.dma_start(
+                out=rows[:].rearrange("q e k -> q (e k)"),
+                in_=s2t_W1_w[r * PIECE : (r + 1) * PIECE, :].rearrange("(q e) k -> q (e k)", e=2),
+            )
+            w1_raw.append(rows)
+        load_tokens(1, 0, 2)
+        load_tokens(2, 0, 2)
+
+        w2_raw = []
+        for r in range(WEIGHT_PIECES):
+            rows = raw.tile([P, 2, H], BF16, tag="raw", name="w2_raw%d" % r)
+            nc.sync.dma_start(
+                out=rows[:],
+                in_=s2t_W_w[r * PIECE : (r + 1) * PIECE, :].rearrange("(i q) k -> q i k", q=P),
+            )
+            w2_raw.append(rows)
+
+        load_tokens(3, 0, 2)
+        for b in range(BATCHES):
+            load_tokens(b, 2, 3)
+
+        w1_codes = keep.tile([P, PASSES, H], U32, align_bytes=64)
+        w1_scales = keep.tile([P, PASSES, H], U8, align_bytes=64)
+        w2_codes = keep.tile([P, PASSES, H], U32, align_bytes=64)
+        w2_scales = keep.tile([P, PASSES, H], U8, align_bytes=64)
+        token_pieces = BATCHES * TOKENS * P // PIECE
+        f_codes = []
+        f_scales = []
+        for s in range(token_pieces):
+            f_codes.append(keep.tile([P, PASSES, PIECE], U32, align_bytes=64, name="f_codes%d" % s))
+            f_scales.append(keep.tile([P, PASSES, PIECE], U8, align_bytes=64, name="f_scales%d" % s))
+
+        pair_lse = []
+        pair_term = []
+        pair_mix = []
+        third_gap = []
+        for b in range(BATCHES):
+            pair_lse.append(keep.tile([P, H], F32, name="pair_lse%d" % b))
+            pair_term.append(keep.tile([P, H], F32, name="pair_term%d" % b))
+            pair_mix.append(keep.tile([P, H], F32, name="pair_mix%d" % b))
+            third_gap.append(keep.tile([P, H], F32, name="third_gap%d" % b))
+
+        def token_rows(s):
+            if s < BATCHES:
+                return [h_rows[s][:, 0, :], h_rows[s][:, 1, :]]
+            first = 2 * (s - BATCHES)
+            return [h_rows[first][:, 2, :], h_rows[first + 1][:, 2, :]]
+
+        def piece_of(b, j):
+            if j < 2:
+                return b, j
+            return BATCHES + b // 2, b % 2
+
+        def transpose_piece(row_tiles, copies):
+            grouped = stage.tile([P, PASSES, PIECE, PACK], BF16, tag="grouped", align_bytes=64)
+            grouped_words = (
+                grouped[:]
+                .rearrange("q g c t -> q (g c t)")
+                .bitcast(F32)
+                .rearrange("q (g c u) -> q g c u", g=PASSES, u=PLANES)
+            )
+            for side in range(2):
+                words = row_tiles[side].bitcast(F32)
+                bank = psum.tile([P, PASSES, PLANES, P], F32, tag="bank")
+                for g in range(PASSES):
+                    for u in range(PLANES):
+                        first = (g * PLANES + u) * P
+                        nc.tensor.transpose(bank[:, g, u, :], words[:, first : first + P], ident[:])
+                copies[side](
+                    out=grouped_words[:, :, side * P : (side + 1) * P, :],
+                    in_=bank[:].rearrange("q g u c -> q g c u"),
+                )
+            return grouped
+
+        def quantise_piece(grouped, codes, scales):
+            for g in range(PASSES):
+                nc.vector.quantize_mx(
+                    out=codes[:, g, :].bitcast(FP8X4),
+                    scales=scales[:, g, :],
+                    in_=grouped[:, g, :, :].rearrange("q c t -> q (c t)"),
+                )
+
+        both_engines = [nc.scalar.copy, nc.vector.tensor_copy]
+        scalar_only = [nc.scalar.copy, nc.scalar.copy]
+        vector_only = [nc.vector.tensor_copy, nc.vector.tensor_copy]
+
+        token_grouped = {}
+        token_codes = {}
+        token_scales = {}
+
+        def transpose_tokens(s, copies):
+            token_grouped[s] = transpose_piece(token_rows(s), copies)
+
+        def quantise_tokens(s):
+            codes = stage.tile([P, PASSES, PIECE], U32, tag="token_codes", align_bytes=64)
+            scales = stage.tile([P, PASSES, PIECE], U8, tag="token_scales", align_bytes=64)
+            quantise_piece(token_grouped[s], codes, scales)
+            token_codes[s] = codes
+            token_scales[s] = scales
+
+        hidden_rows_of = {}
+
+        def hidden_rows(s):
+            f_rows = hidden.tile([P, ROW_TILES, PIECE], BF16, tag="f_rows")
+            hidden_rows_of[s] = f_rows
+            for m in range(ROW_TILES):
+                bank = psum.tile([P, BANK], F32, tag="bank")
+                for g in range(PASSES):
+                    nc.tensor.matmul_mx(
+                        out=bank[:, 0:PIECE],
+                        lhsT=w1_codes[:, g, m * P : (m + 1) * P].bitcast(FP8X4),
+                        lhsT_scale=w1_scales[:, g, m * P : (m + 1) * P],
+                        rhs=token_codes[s][:, g, :].bitcast(FP8X4),
+                        rhs_scale=token_scales[s][:, g, :],
+                        start=(g == 0),
+                        stop=(g == PASSES - 1),
+                    )
+                nc.scalar.activation(
+                    out=f_rows[:, m, :],
+                    in_=bank[:, 0:PIECE],
+                    func=ACT.Relu,
+                    bias=bias[:, m : m + 1],
+                    scale=1.0,
+                )
+
+        def hidden_codes(s):
+            f_rows = hidden_rows_of[s]
+            f_grouped = hidden.tile([P, PASSES, PIECE, PACK], BF16, tag="f_grouped", align_bytes=64)
+            for g in range(PASSES):
+                nc.vector.tensor_copy(
+                    out=f_grouped[:, g, :, :].rearrange("q (c i) t -> q c t i", i=RUN),
+                    in_=f_rows[:, g * PACK : (g + 1) * PACK, :].rearrange("q t (c i) -> q c t i", i=RUN),
+                )
+            quantise_piece(f_grouped, f_codes[s], f_scales[s])
+
+        def scores(b, j, half):
+            s, side = piece_of(b, j)
+            bank = psum.tile([P, BANK], F32, tag="bank")
+            for g in range(PASSES):
+                nc.tensor.matmul_mx(
+                    out=bank[:],
+                    lhsT=f_codes[s][:, g, side * P : (side + 1) * P].bitcast(FP8X4),
+                    lhsT_scale=f_scales[s][:, g, side * P : (side + 1) * P],
+                    rhs=w2_codes[:, g, half * BANK : (half + 1) * BANK].bitcast(FP8X4),
+                    rhs_scale=w2_scales[:, g, half * BANK : (half + 1) * BANK],
+                    start=(g == 0),
+                    stop=(g == PASSES - 1),
+                )
+            return bank
+
+        tanh_lead = {}
+        half_gap = {}
+
+        def scores_first_two(b):
+            z0 = []
+            z1 = []
+            for half in range(HALVES):
+                cols = slice(half * BANK, (half + 1) * BANK)
+                z0.append(scores(b, 0, half))
+                z1.append(scores(b, 1, half))
+                gap = psum_gap.tile([P, BANK], F32, tag="gap")
+                nc.tensor.matmul(out=gap[:], lhsT=half_plus[:], rhs=h_rows[b][:, 1, cols], start=True, stop=False)
+                nc.tensor.matmul(out=gap[:], lhsT=half_minus[:], rhs=h_rows[b][:, 0, cols], start=False, stop=True)
+                half_gap[(b, half)] = gap
+            z0_copy = []
+            for half in range(HALVES):
+                first = work.tile([P, BANK], F32, tag="first")
+                nc.scalar.copy(out=first[:], in_=z0[half][:])
+                z0_copy.append(first)
+            leads = []
+            for half in range(HALVES):
+                cols = slice(half * BANK, (half + 1) * BANK)
+                lead = work.tile([P, BANK], F32, tag="lead")
+                nc.vector.tensor_tensor(out=lead[:], in0=z1[half][:], in1=z0_copy[half][:], op=ALU.subtract)
+                nc.vector.tensor_tensor(out=pair_lse[b][:, cols], in0=z1[half][:], in1=z0_copy[half][:], op=ALU.max)
+                leads.append(lead)
+            tanh_pair = work.tile([P, H], F32, tag="tanh_pair")
+            for half in range(HALVES):
+                cols = slice(half * BANK, (half + 1) * BANK)
+                nc.scalar.activation(out=tanh_pair[:, cols], in_=leads[half][:], func=ACT.Tanh, scale=0.5)
+            nc.scalar.activation(out=pair_term[b][:], in_=tanh_pair[:], func=ACT.Abs)
+            tanh_lead[b] = tanh_pair
+
+        def blend_first_two(b):
+            for half in range(HALVES):
+                cols = slice(half * BANK, (half + 1) * BANK)
+                nc.vector.scalar_tensor_tensor(
+                    out=pair_mix[b][:, cols],
+                    in0=tanh_lead[b][:, cols],
+                    scalar=1.0,
+                    in1=half_gap[(b, half)][:],
+                    op0=ALU.add,
+                    op1=ALU.mult,
+                )
+            nc.vector.tensor_tensor(out=pair_mix[b][:], in0=pair_mix[b][:], in1=h_rows[b][:, 0, :], op=ALU.add)
+
+        tanh_third = {}
+
+        def third_score(b, half):
+            cols = slice(half * BANK, (half + 1) * BANK)
+            z2 = scores(b, 2, half)
+            lead = work.tile([P, BANK], F32, tag="third_lead", bufs=3)
+            nc.vector.tensor_tensor(out=lead[:], in0=z2[:], in1=pair_lse[b][:, cols], op=ALU.subtract)
+            tanh_last = work.tile([P, BANK], F32, tag="tanh_last", bufs=LAG + 2)
+            nc.scalar.activation(out=tanh_last[:], in_=lead[:], func=ACT.Tanh, scale=0.5)
+            tanh_third[(b, half)] = tanh_last
+
+        def finish(b, half):
+            cols = slice(half * BANK, (half + 1) * BANK)
+            step = work.tile([P, BANK], F32, tag="step")
+            nc.vector.scalar_tensor_tensor(
+                out=step[:],
+                in0=tanh_third[(b, half)][:],
+                scalar=1.0,
+                in1=third_gap[b][:, cols],
+                op0=ALU.add,
+                op1=ALU.mult,
+            )
+            result = work.tile([P, BANK], F32, tag="result", bufs=3)
+            nc.vector.scalar_tensor_tensor(
+                out=result[:],
+                in0=step[:],
+                scalar=0.5,
+                in1=pair_mix[b][:, cols],
+                op0=ALU.mult,
+                op1=ALU.add,
+            )
+            nc.sync.dma_start(out=out_flat[b * P : (b + 1) * P, cols], in_=result[:])
+
+        def prepare_weights(rows, codes, scales, r, copies):
+            cols = slice(r * PIECE, (r + 1) * PIECE)
+            grouped = transpose_piece([rows[r][:, 0, :], rows[r][:, 1, :]], copies)
+            quantise_piece(grouped, codes[:, :, cols], scales[:, :, cols])
+
+        transpose_tokens(0, both_engines)
+        quantise_tokens(0)
+        spread_bias()
+        for r in range(WEIGHT_PIECES):
+            prepare_weights(w1_raw, w1_codes, w1_scales, r, scalar_only)
+        transpose_tokens(1, scalar_only)
+        quantise_tokens(1)
+        hidden_rows(0)
+        prepare_weights(w2_raw, w2_codes, w2_scales, 0, vector_only)
+        hidden_codes(0)
+        for r in range(1, WEIGHT_PIECES):
+            prepare_weights(w2_raw, w2_codes, w2_scales, r, scalar_only)
+
+        for b in range(BATCHES):
+            hidden_rows(b + 1)
+            transpose_tokens(b + 2, scalar_only)
+            if b > 0:
+                blend_first_two(b - 1)
+            hidden_codes(b + 1)
+            scores_first_two(b)
+            quantise_tokens(b + 2)
+        hidden_rows(BATCHES + 1)
+        blend_first_two(BATCHES - 1)
+        hidden_codes(BATCHES + 1)
+
+        for b in range(BATCHES):
+            nc.vector.tensor_tensor(out=third_gap[b][:], in0=h_rows[b][:, 2, :], in1=pair_mix[b][:], op=ALU.subtract)
+        for b in range(BATCHES):
+            nc.scalar.activation(out=pair_term[b][:], in_=pair_term[b][:], func=ACT.Ln, scale=0.5, bias=half_col[:])
+            nc.vector.tensor_tensor(out=pair_lse[b][:], in0=pair_lse[b][:], in1=pair_term[b][:], op=ALU.subtract)
+
+        halves = [(b, half) for b in range(BATCHES) for half in range(HALVES)]
+        for i in range(len(halves) + LAG):
+            if i < len(halves):
+                third_score(halves[i][0], halves[i][1])
+            if i >= LAG:
+                finish(halves[i - LAG][0], halves[i - LAG][1])

@@ -24,7 +24,6 @@ ROW_TILES = H // P
 BANK = 512
 HALVES = H // BANK
 RUN = 4
-LAG = 2
 
 FLOPS = 2 * 2 * BATCHES * P * TOKENS * H * H
 
@@ -41,8 +40,8 @@ def tile_blocksa_pa_kernel(tc, h, s2t_W1_w, s2t_W1_b, s2t_W_w, out):
         stage = stack.enter_context(tc.tile_pool(name="stage", bufs=3))
         hidden = stack.enter_context(tc.tile_pool(name="hidden", bufs=2))
         work = stack.enter_context(tc.tile_pool(name="work", bufs=2))
-        psum = stack.enter_context(tc.psum_pool(name="psum", bufs=6))
-        psum_gap = stack.enter_context(tc.psum_pool(name="psum_gap", bufs=2))
+        psum = stack.enter_context(tc.psum_pool(name="psum", bufs=4))
+        psum_gap = stack.enter_context(tc.psum_pool(name="psum_gap", bufs=4))
         stack.enter_context(tc.manual_schedule())
 
         bias_rows = consts.tile([P, 2 * P], BF16)
@@ -57,10 +56,11 @@ def tile_blocksa_pa_kernel(tc, h, s2t_W1_w, s2t_W1_b, s2t_W_w, out):
 
         ident = consts.tile([P, P], F32)
         make_identity(nc, ident[:])
-        half_plus = consts.tile([P, P], BF16)
-        nc.vector.tensor_scalar_mul(out=half_plus[:], in0=ident[:], scalar1=0.5)
-        half_minus = consts.tile([P, P], BF16)
-        nc.vector.tensor_scalar_mul(out=half_minus[:], in0=ident[:], scalar1=-0.5)
+        diagonal = {}
+        for value in (0.25, -0.25, 0.5, -0.5):
+            scaled = consts.tile([P, P], BF16, name="diagonal%d" % len(diagonal))
+            nc.vector.tensor_scalar_mul(out=scaled[:], in0=ident[:], scalar1=value)
+            diagonal[value] = scaled
 
         def spread_bias():
             bias_bank = psum.tile([P, BANK], F32, tag="bank")
@@ -121,13 +121,11 @@ def tile_blocksa_pa_kernel(tc, h, s2t_W1_w, s2t_W1_b, s2t_W_w, out):
 
         pair_lse = []
         pair_term = []
-        pair_mix = []
-        third_gap = []
+        offset_half = []
         for b in range(BATCHES):
             pair_lse.append(keep.tile([P, H], F32, name="pair_lse%d" % b))
             pair_term.append(keep.tile([P, H], F32, name="pair_term%d" % b))
-            pair_mix.append(keep.tile([P, H], F32, name="pair_mix%d" % b))
-            third_gap.append(keep.tile([P, H], F32, name="third_gap%d" % b))
+            offset_half.append(keep.tile([P, H], F32, name="offset_half%d" % b))
 
         def token_rows(s):
             if s < BATCHES:
@@ -140,7 +138,19 @@ def tile_blocksa_pa_kernel(tc, h, s2t_W1_w, s2t_W1_b, s2t_W_w, out):
                 return b, j
             return BATCHES + b // 2, b % 2
 
-        def transpose_piece(row_tiles, copies):
+        def transpose_piece(row_tiles):
+            banks = []
+            for side in range(2):
+                words = row_tiles[side].bitcast(F32)
+                bank = psum.tile([P, PASSES, PLANES, P], F32, tag="bank")
+                for g in range(PASSES):
+                    for u in range(PLANES):
+                        first = (g * PLANES + u) * P
+                        nc.tensor.transpose(bank[:, g, u, :], words[:, first : first + P], ident[:])
+                banks.append(bank)
+            return banks
+
+        def copy_piece(banks, copies):
             grouped = stage.tile([P, PASSES, PIECE, PACK], BF16, tag="grouped", align_bytes=64)
             grouped_words = (
                 grouped[:]
@@ -149,15 +159,9 @@ def tile_blocksa_pa_kernel(tc, h, s2t_W1_w, s2t_W1_b, s2t_W_w, out):
                 .rearrange("q (g c u) -> q g c u", g=PASSES, u=PLANES)
             )
             for side in range(2):
-                words = row_tiles[side].bitcast(F32)
-                bank = psum.tile([P, PASSES, PLANES, P], F32, tag="bank")
-                for g in range(PASSES):
-                    for u in range(PLANES):
-                        first = (g * PLANES + u) * P
-                        nc.tensor.transpose(bank[:, g, u, :], words[:, first : first + P], ident[:])
                 copies[side](
                     out=grouped_words[:, :, side * P : (side + 1) * P, :],
-                    in_=bank[:].rearrange("q g u c -> q g c u"),
+                    in_=banks[side][:].rearrange("q g u c -> q g c u"),
                 )
             return grouped
 
@@ -173,12 +177,16 @@ def tile_blocksa_pa_kernel(tc, h, s2t_W1_w, s2t_W1_b, s2t_W_w, out):
         scalar_only = [nc.scalar.copy, nc.scalar.copy]
         vector_only = [nc.vector.tensor_copy, nc.vector.tensor_copy]
 
+        token_banks = {}
         token_grouped = {}
         token_codes = {}
         token_scales = {}
 
-        def transpose_tokens(s, copies):
-            token_grouped[s] = transpose_piece(token_rows(s), copies)
+        def transpose_tokens(s):
+            token_banks[s] = transpose_piece(token_rows(s))
+
+        def copy_tokens(s, copies):
+            token_grouped[s] = copy_piece(token_banks[s], copies)
 
         def quantise_tokens(s):
             codes = stage.tile([P, PASSES, PIECE], U32, tag="token_codes", align_bytes=64)
@@ -238,7 +246,13 @@ def tile_blocksa_pa_kernel(tc, h, s2t_W1_w, s2t_W1_b, s2t_W_w, out):
             return bank
 
         tanh_lead = {}
-        half_gap = {}
+        gaps = {}
+
+        def difference(b, j_plus, j_minus, weight, cols):
+            gap = psum_gap.tile([P, BANK], F32, tag="gap")
+            nc.tensor.matmul(out=gap[:], lhsT=diagonal[weight][:], rhs=h_rows[b][:, j_plus, cols], start=True, stop=False)
+            nc.tensor.matmul(out=gap[:], lhsT=diagonal[-weight][:], rhs=h_rows[b][:, j_minus, cols], start=False, stop=True)
+            return gap
 
         def scores_first_two(b):
             z0 = []
@@ -247,10 +261,7 @@ def tile_blocksa_pa_kernel(tc, h, s2t_W1_w, s2t_W1_b, s2t_W_w, out):
                 cols = slice(half * BANK, (half + 1) * BANK)
                 z0.append(scores(b, 0, half))
                 z1.append(scores(b, 1, half))
-                gap = psum_gap.tile([P, BANK], F32, tag="gap")
-                nc.tensor.matmul(out=gap[:], lhsT=half_plus[:], rhs=h_rows[b][:, 1, cols], start=True, stop=False)
-                nc.tensor.matmul(out=gap[:], lhsT=half_minus[:], rhs=h_rows[b][:, 0, cols], start=False, stop=True)
-                half_gap[(b, half)] = gap
+                gaps[(b, half)] = (difference(b, 1, 0, 0.25, cols), difference(b, 0, 2, 0.5, cols))
             z0_copy = []
             for half in range(HALVES):
                 first = work.tile([P, BANK], F32, tag="first")
@@ -267,94 +278,102 @@ def tile_blocksa_pa_kernel(tc, h, s2t_W1_w, s2t_W1_b, s2t_W_w, out):
             for half in range(HALVES):
                 cols = slice(half * BANK, (half + 1) * BANK)
                 nc.scalar.activation(out=tanh_pair[:, cols], in_=leads[half][:], func=ACT.Tanh, scale=0.5)
-            nc.scalar.activation(out=pair_term[b][:], in_=tanh_pair[:], func=ACT.Abs)
+            for half in range(HALVES):
+                cols = slice(half * BANK, (half + 1) * BANK)
+                nc.scalar.activation(out=pair_term[b][:, cols], in_=tanh_pair[:, cols], func=ACT.Abs)
             tanh_lead[b] = tanh_pair
 
         def blend_first_two(b):
+            parts = []
             for half in range(HALVES):
                 cols = slice(half * BANK, (half + 1) * BANK)
+                part = work.tile([P, BANK], F32, tag="part")
                 nc.vector.scalar_tensor_tensor(
-                    out=pair_mix[b][:, cols],
+                    out=part[:],
                     in0=tanh_lead[b][:, cols],
                     scalar=1.0,
-                    in1=half_gap[(b, half)][:],
+                    in1=gaps[(b, half)][0][:],
                     op0=ALU.add,
                     op1=ALU.mult,
                 )
-            nc.vector.tensor_tensor(out=pair_mix[b][:], in0=pair_mix[b][:], in1=h_rows[b][:, 0, :], op=ALU.add)
+                parts.append(part)
+            for half in range(HALVES):
+                cols = slice(half * BANK, (half + 1) * BANK)
+                nc.vector.tensor_tensor(out=offset_half[b][:, cols], in0=parts[half][:], in1=gaps[(b, half)][1][:], op=ALU.add)
 
         tanh_third = {}
 
-        def third_score(b, half):
-            cols = slice(half * BANK, (half + 1) * BANK)
-            z2 = scores(b, 2, half)
-            lead = work.tile([P, BANK], F32, tag="third_lead", bufs=3)
-            nc.vector.tensor_tensor(out=lead[:], in0=z2[:], in1=pair_lse[b][:, cols], op=ALU.subtract)
-            tanh_last = work.tile([P, BANK], F32, tag="tanh_last", bufs=LAG + 2)
-            nc.scalar.activation(out=tanh_last[:], in_=lead[:], func=ACT.Tanh, scale=0.5)
-            tanh_third[(b, half)] = tanh_last
+        def third_score(b):
+            for half in range(HALVES):
+                cols = slice(half * BANK, (half + 1) * BANK)
+                z2 = scores(b, 2, half)
+                lead = work.tile([P, BANK], F32, tag="third_lead")
+                nc.vector.tensor_tensor(out=lead[:], in0=pair_lse[b][:, cols], in1=z2[:], op=ALU.subtract)
+                tanh_last = work.tile([P, BANK], F32, tag="tanh_last", bufs=2 * HALVES)
+                nc.scalar.activation(out=tanh_last[:], in_=lead[:], func=ACT.Tanh, scale=0.5)
+                tanh_third[(b, half)] = tanh_last
 
-        def finish(b, half):
-            cols = slice(half * BANK, (half + 1) * BANK)
-            step = work.tile([P, BANK], F32, tag="step")
-            nc.vector.scalar_tensor_tensor(
-                out=step[:],
-                in0=tanh_third[(b, half)][:],
-                scalar=1.0,
-                in1=third_gap[b][:, cols],
-                op0=ALU.add,
-                op1=ALU.mult,
-            )
-            result = work.tile([P, BANK], F32, tag="result", bufs=3)
-            nc.vector.scalar_tensor_tensor(
-                out=result[:],
-                in0=step[:],
-                scalar=0.5,
-                in1=pair_mix[b][:, cols],
-                op0=ALU.mult,
-                op1=ALU.add,
-            )
-            nc.sync.dma_start(out=out_flat[b * P : (b + 1) * P, cols], in_=result[:])
+        def finish(b):
+            steps = []
+            for half in range(HALVES):
+                cols = slice(half * BANK, (half + 1) * BANK)
+                step = work.tile([P, BANK], F32, tag="step")
+                nc.vector.scalar_tensor_tensor(
+                    out=step[:],
+                    in0=tanh_third[(b, half)][:],
+                    scalar=1.0,
+                    in1=offset_half[b][:, cols],
+                    op0=ALU.add,
+                    op1=ALU.mult,
+                )
+                steps.append(step)
+            for half in range(HALVES):
+                cols = slice(half * BANK, (half + 1) * BANK)
+                result = work.tile([P, BANK], F32, tag="result", bufs=2 * HALVES)
+                nc.vector.tensor_tensor(out=result[:], in0=steps[half][:], in1=h_rows[b][:, 2, cols], op=ALU.add)
+                nc.sync.dma_start(out=out_flat[b * P : (b + 1) * P, cols], in_=result[:])
 
         def prepare_weights(rows, codes, scales, r, copies):
             cols = slice(r * PIECE, (r + 1) * PIECE)
-            grouped = transpose_piece([rows[r][:, 0, :], rows[r][:, 1, :]], copies)
+            grouped = copy_piece(transpose_piece([rows[r][:, 0, :], rows[r][:, 1, :]]), copies)
             quantise_piece(grouped, codes[:, :, cols], scales[:, :, cols])
 
-        transpose_tokens(0, both_engines)
+        transpose_tokens(0)
+        copy_tokens(0, both_engines)
         quantise_tokens(0)
         spread_bias()
         for r in range(WEIGHT_PIECES):
             prepare_weights(w1_raw, w1_codes, w1_scales, r, scalar_only)
-        transpose_tokens(1, scalar_only)
+        transpose_tokens(1)
+        copy_tokens(1, scalar_only)
         quantise_tokens(1)
         hidden_rows(0)
         prepare_weights(w2_raw, w2_codes, w2_scales, 0, vector_only)
         hidden_codes(0)
         for r in range(1, WEIGHT_PIECES):
             prepare_weights(w2_raw, w2_codes, w2_scales, r, scalar_only)
+        transpose_tokens(2)
 
         for b in range(BATCHES):
+            copy_tokens(b + 2, both_engines)
             hidden_rows(b + 1)
-            transpose_tokens(b + 2, scalar_only)
             if b > 0:
                 blend_first_two(b - 1)
+            quantise_tokens(b + 2)
             hidden_codes(b + 1)
             scores_first_two(b)
-            quantise_tokens(b + 2)
+            if b + 3 < token_pieces:
+                transpose_tokens(b + 3)
         hidden_rows(BATCHES + 1)
         blend_first_two(BATCHES - 1)
         hidden_codes(BATCHES + 1)
 
         for b in range(BATCHES):
-            nc.vector.tensor_tensor(out=third_gap[b][:], in0=h_rows[b][:, 2, :], in1=pair_mix[b][:], op=ALU.subtract)
-        for b in range(BATCHES):
             nc.scalar.activation(out=pair_term[b][:], in_=pair_term[b][:], func=ACT.Ln, scale=0.5, bias=half_col[:])
             nc.vector.tensor_tensor(out=pair_lse[b][:], in0=pair_lse[b][:], in1=pair_term[b][:], op=ALU.subtract)
 
-        halves = [(b, half) for b in range(BATCHES) for half in range(HALVES)]
-        for i in range(len(halves) + LAG):
-            if i < len(halves):
-                third_score(halves[i][0], halves[i][1])
-            if i >= LAG:
-                finish(halves[i - LAG][0], halves[i - LAG][1])
+        for b in range(BATCHES + 1):
+            if b < BATCHES:
+                third_score(b)
+            if b > 0:
+                finish(b - 1)

@@ -40,8 +40,8 @@ def tile_blocksa_pa_kernel(tc, h, s2t_W1_w, s2t_W1_b, s2t_W_w, out):
         stage = stack.enter_context(tc.tile_pool(name="stage", bufs=3))
         hidden = stack.enter_context(tc.tile_pool(name="hidden", bufs=2))
         work = stack.enter_context(tc.tile_pool(name="work", bufs=2))
-        psum = stack.enter_context(tc.psum_pool(name="psum", bufs=4))
-        psum_gap = stack.enter_context(tc.psum_pool(name="psum_gap", bufs=4))
+        psum = stack.enter_context(tc.psum_pool(name="psum", bufs=6))
+        psum_gap = stack.enter_context(tc.psum_pool(name="psum_gap", bufs=2))
         stack.enter_context(tc.manual_schedule())
 
         bias_rows = consts.tile([P, 2 * P], BF16)
@@ -57,7 +57,7 @@ def tile_blocksa_pa_kernel(tc, h, s2t_W1_w, s2t_W1_b, s2t_W_w, out):
         ident = consts.tile([P, P], F32)
         make_identity(nc, ident[:])
         diagonal = {}
-        for value in (0.25, -0.25, 0.5, -0.5):
+        for value in (0.5, -0.5):
             scaled = consts.tile([P, P], BF16, name="diagonal%d" % len(diagonal))
             nc.vector.tensor_scalar_mul(out=scaled[:], in0=ident[:], scalar1=value)
             diagonal[value] = scaled
@@ -121,11 +121,11 @@ def tile_blocksa_pa_kernel(tc, h, s2t_W1_w, s2t_W1_b, s2t_W_w, out):
 
         pair_lse = []
         pair_term = []
-        offset_half = []
+        offset = []
         for b in range(BATCHES):
             pair_lse.append(keep.tile([P, H], F32, name="pair_lse%d" % b))
             pair_term.append(keep.tile([P, H], F32, name="pair_term%d" % b))
-            offset_half.append(keep.tile([P, H], F32, name="offset_half%d" % b))
+            offset.append(keep.tile([P, H], F32, name="offset%d" % b))
 
         def token_rows(s):
             if s < BATCHES:
@@ -248,11 +248,13 @@ def tile_blocksa_pa_kernel(tc, h, s2t_W1_w, s2t_W1_b, s2t_W_w, out):
         tanh_lead = {}
         gaps = {}
 
-        def difference(b, j_plus, j_minus, weight, cols):
+        def differences(b, cols):
             gap = psum_gap.tile([P, BANK], F32, tag="gap")
-            nc.tensor.matmul(out=gap[:], lhsT=diagonal[weight][:], rhs=h_rows[b][:, j_plus, cols], start=True, stop=False)
-            nc.tensor.matmul(out=gap[:], lhsT=diagonal[-weight][:], rhs=h_rows[b][:, j_minus, cols], start=False, stop=True)
-            return gap
+            nc.tensor.matmul(out=gap[:], lhsT=diagonal[0.5][:], rhs=h_rows[b][:, 1, cols], start=True, stop=False)
+            nc.tensor.matmul(out=gap[:], lhsT=diagonal[-0.5][:], rhs=h_rows[b][:, 0, cols], start=False, stop=True)
+            base = work.tile([P, BANK], F32, tag="base", bufs=2 * HALVES)
+            nc.gpsimd.tensor_tensor(out=base[:], in0=h_rows[b][:, 0, cols], in1=h_rows[b][:, 2, cols], op=ALU.subtract)
+            return gap, base
 
         def scores_first_two(b):
             z0 = []
@@ -261,7 +263,7 @@ def tile_blocksa_pa_kernel(tc, h, s2t_W1_w, s2t_W1_b, s2t_W_w, out):
                 cols = slice(half * BANK, (half + 1) * BANK)
                 z0.append(scores(b, 0, half))
                 z1.append(scores(b, 1, half))
-                gaps[(b, half)] = (difference(b, 1, 0, 0.25, cols), difference(b, 0, 2, 0.5, cols))
+                gaps[(b, half)] = differences(b, cols)
             z0_copy = []
             for half in range(HALVES):
                 first = work.tile([P, BANK], F32, tag="first")
@@ -299,7 +301,7 @@ def tile_blocksa_pa_kernel(tc, h, s2t_W1_w, s2t_W1_b, s2t_W_w, out):
                 parts.append(part)
             for half in range(HALVES):
                 cols = slice(half * BANK, (half + 1) * BANK)
-                nc.vector.tensor_tensor(out=offset_half[b][:, cols], in0=parts[half][:], in1=gaps[(b, half)][1][:], op=ALU.add)
+                nc.vector.tensor_tensor(out=offset[b][:, cols], in0=parts[half][:], in1=gaps[(b, half)][1][:], op=ALU.add)
 
         tanh_third = {}
 
@@ -322,7 +324,7 @@ def tile_blocksa_pa_kernel(tc, h, s2t_W1_w, s2t_W1_b, s2t_W_w, out):
                     out=step[:],
                     in0=tanh_third[(b, half)][:],
                     scalar=1.0,
-                    in1=offset_half[b][:, cols],
+                    in1=offset[b][:, cols],
                     op0=ALU.add,
                     op1=ALU.mult,
                 )
@@ -330,7 +332,14 @@ def tile_blocksa_pa_kernel(tc, h, s2t_W1_w, s2t_W1_b, s2t_W_w, out):
             for half in range(HALVES):
                 cols = slice(half * BANK, (half + 1) * BANK)
                 result = work.tile([P, BANK], F32, tag="result", bufs=2 * HALVES)
-                nc.vector.tensor_tensor(out=result[:], in0=steps[half][:], in1=h_rows[b][:, 2, cols], op=ALU.add)
+                nc.vector.scalar_tensor_tensor(
+                    out=result[:],
+                    in0=steps[half][:],
+                    scalar=0.5,
+                    in1=h_rows[b][:, 2, cols],
+                    op0=ALU.mult,
+                    op1=ALU.add,
+                )
                 nc.sync.dma_start(out=out_flat[b * P : (b + 1) * P, cols], in_=result[:])
 
         def prepare_weights(rows, codes, scales, r, copies):

@@ -18,8 +18,10 @@ H = 1024
 PACK = 4
 PASSES = H // (P * PACK)
 PLANES = 2
-PIECE = 2 * P
+SIDES = 2
+PIECE = SIDES * P
 WEIGHT_PIECES = H // PIECE
+TOKEN_PIECES = BATCHES * TOKENS * P // PIECE
 ROW_TILES = H // P
 BANK = 512
 HALVES = H // BANK
@@ -76,46 +78,45 @@ def tile_blocksa_pa_kernel(tc, h, s2t_W1_w, s2t_W1_b, s2t_W_w, out):
         for b in range(BATCHES):
             h_rows.append(keep.tile([P, TOKENS, H], BF16, name="h_rows%d" % b))
 
-        def load_tokens(b, first, last):
+        def load_tokens(b, j_from, j_to):
             nc.sync.dma_start(
-                out=h_rows[b][:, first:last, :].rearrange("n j k -> n (j k)"),
-                in_=h_flat[b * P : (b + 1) * P, first * H : last * H],
+                out=h_rows[b][:, j_from:j_to, :].rearrange("n j k -> n (j k)"),
+                in_=h_flat[b * P : (b + 1) * P, j_from * H : j_to * H],
             )
 
-        load_tokens(0, 0, 2)
+        load_tokens(0, 0, SIDES)
 
         w1_raw = []
         for r in range(WEIGHT_PIECES):
-            rows = raw.tile([P, 2, H], BF16, tag="raw", name="w1_raw%d" % r)
+            rows = raw.tile([P, SIDES, H], BF16, tag="raw", name="w1_raw%d" % r)
             nc.sync.dma_start(
                 out=rows[:].rearrange("q e k -> q (e k)"),
-                in_=s2t_W1_w[r * PIECE : (r + 1) * PIECE, :].rearrange("(q e) k -> q (e k)", e=2),
+                in_=s2t_W1_w[r * PIECE : (r + 1) * PIECE, :].rearrange("(q e) k -> q (e k)", e=SIDES),
             )
             w1_raw.append(rows)
-        load_tokens(1, 0, 2)
-        load_tokens(2, 0, 2)
+        load_tokens(1, 0, SIDES)
+        load_tokens(2, 0, SIDES)
 
         w2_raw = []
         for r in range(WEIGHT_PIECES):
-            rows = raw.tile([P, 2, H], BF16, tag="raw", name="w2_raw%d" % r)
+            rows = raw.tile([P, SIDES, H], BF16, tag="raw", name="w2_raw%d" % r)
             nc.sync.dma_start(
                 out=rows[:],
                 in_=s2t_W_w[r * PIECE : (r + 1) * PIECE, :].rearrange("(i q) k -> q i k", q=P),
             )
             w2_raw.append(rows)
 
-        load_tokens(3, 0, 2)
+        load_tokens(3, 0, SIDES)
         for b in range(BATCHES):
-            load_tokens(b, 2, 3)
+            load_tokens(b, SIDES, TOKENS)
 
         w1_codes = keep.tile([P, PASSES, H], U32, align_bytes=64)
         w1_scales = keep.tile([P, PASSES, H], U8, align_bytes=64)
         w2_codes = keep.tile([P, PASSES, H], U32, align_bytes=64)
         w2_scales = keep.tile([P, PASSES, H], U8, align_bytes=64)
-        token_pieces = BATCHES * TOKENS * P // PIECE
         f_codes = []
         f_scales = []
-        for s in range(token_pieces):
+        for s in range(TOKEN_PIECES):
             f_codes.append(keep.tile([P, PASSES, PIECE], U32, align_bytes=64, name="f_codes%d" % s))
             f_scales.append(keep.tile([P, PASSES, PIECE], U8, align_bytes=64, name="f_scales%d" % s))
 
@@ -130,23 +131,25 @@ def tile_blocksa_pa_kernel(tc, h, s2t_W1_w, s2t_W1_b, s2t_W_w, out):
         def token_rows(s):
             if s < BATCHES:
                 return [h_rows[s][:, 0, :], h_rows[s][:, 1, :]]
-            first = 2 * (s - BATCHES)
-            return [h_rows[first][:, 2, :], h_rows[first + 1][:, 2, :]]
+            batch = SIDES * (s - BATCHES)
+            return [h_rows[batch][:, 2, :], h_rows[batch + 1][:, 2, :]]
 
         def piece_of(b, j):
-            if j < 2:
+            if j < SIDES:
                 return b, j
-            return BATCHES + b // 2, b % 2
+            return BATCHES + b // SIDES, b % SIDES
+
+        token_0_sides = [piece_of(b, 0) for b in range(BATCHES)]
 
         def transpose_piece(row_tiles):
             banks = []
-            for side in range(2):
+            for side in range(SIDES):
                 words = row_tiles[side].bitcast(F32)
                 bank = psum.tile([P, PASSES, PLANES, P], F32, tag="bank")
                 for g in range(PASSES):
                     for u in range(PLANES):
-                        first = (g * PLANES + u) * P
-                        nc.tensor.transpose(bank[:, g, u, :], words[:, first : first + P], ident[:])
+                        start = (g * PLANES + u) * P
+                        nc.tensor.transpose(bank[:, g, u, :], words[:, start : start + P], ident[:])
                 banks.append(bank)
             return banks
 
@@ -158,7 +161,7 @@ def tile_blocksa_pa_kernel(tc, h, s2t_W1_w, s2t_W1_b, s2t_W_w, out):
                 .bitcast(F32)
                 .rearrange("q (g c u) -> q g c u", g=PASSES, u=PLANES)
             )
-            for side in range(2):
+            for side in range(SIDES):
                 copies[side](
                     out=grouped_words[:, :, side * P : (side + 1) * P, :],
                     in_=banks[side][:].rearrange("q g u c -> q g c u"),
@@ -224,29 +227,34 @@ def tile_blocksa_pa_kernel(tc, h, s2t_W1_w, s2t_W1_b, s2t_W_w, out):
             f_rows = hidden_rows_of[s]
             f_grouped = hidden.tile([P, PASSES, PIECE, PACK], BF16, tag="f_grouped", align_bytes=64)
             for g in range(PASSES):
-                nc.vector.tensor_copy(
-                    out=f_grouped[:, g, :, :].rearrange("q (c i) t -> q c t i", i=RUN),
-                    in_=f_rows[:, g * PACK : (g + 1) * PACK, :].rearrange("q t (c i) -> q c t i", i=RUN),
-                )
+                for side in range(SIDES):
+                    cols = slice(side * P, (side + 1) * P)
+                    grouped_side = f_grouped[:, g, cols, :].rearrange("q (c i) t -> q c t i", i=RUN)
+                    rows_side = f_rows[:, g * PACK : (g + 1) * PACK, cols].rearrange("q t (c i) -> q c t i", i=RUN)
+                    if (s, side) in token_0_sides:
+                        nc.vector.tensor_scalar_mul(out=grouped_side, in0=rows_side, scalar1=-1.0)
+                    else:
+                        nc.vector.tensor_copy(out=grouped_side, in_=rows_side)
             quantise_piece(f_grouped, f_codes[s], f_scales[s])
 
-        def scores(b, j, half):
-            s, side = piece_of(b, j)
+        def score_lead(b, j, half):
             bank = psum.tile([P, BANK], F32, tag="bank")
-            for g in range(PASSES):
-                nc.tensor.matmul_mx(
-                    out=bank[:],
-                    lhsT=f_codes[s][:, g, side * P : (side + 1) * P].bitcast(FP8X4),
-                    lhsT_scale=f_scales[s][:, g, side * P : (side + 1) * P],
-                    rhs=w2_codes[:, g, half * BANK : (half + 1) * BANK].bitcast(FP8X4),
-                    rhs_scale=w2_scales[:, g, half * BANK : (half + 1) * BANK],
-                    start=(g == 0),
-                    stop=(g == PASSES - 1),
-                )
+            for token in (j, 0):
+                s, side = piece_of(b, token)
+                for g in range(PASSES):
+                    nc.tensor.matmul_mx(
+                        out=bank[:],
+                        lhsT=f_codes[s][:, g, side * P : (side + 1) * P].bitcast(FP8X4),
+                        lhsT_scale=f_scales[s][:, g, side * P : (side + 1) * P],
+                        rhs=w2_codes[:, g, half * BANK : (half + 1) * BANK].bitcast(FP8X4),
+                        rhs_scale=w2_scales[:, g, half * BANK : (half + 1) * BANK],
+                        start=(token == j and g == 0),
+                        stop=(token == 0 and g == PASSES - 1),
+                    )
             return bank
 
         tanh_lead = {}
-        gaps = {}
+        h_differences = {}
 
         def differences(b, cols):
             gap = psum_gap.tile([P, BANK], F32, tag="gap")
@@ -256,34 +264,25 @@ def tile_blocksa_pa_kernel(tc, h, s2t_W1_w, s2t_W1_b, s2t_W_w, out):
             nc.gpsimd.tensor_tensor(out=base[:], in0=h_rows[b][:, 0, cols], in1=h_rows[b][:, 2, cols], op=ALU.subtract)
             return gap, base
 
-        def scores_first_two(b):
-            z0 = []
-            z1 = []
+        d1_banks = {}
+
+        def first_scores(b):
+            for half in range(HALVES):
+                d1_banks[(b, half)] = score_lead(b, 1, half)
             for half in range(HALVES):
                 cols = slice(half * BANK, (half + 1) * BANK)
-                z0.append(scores(b, 0, half))
-                z1.append(scores(b, 1, half))
-                gaps[(b, half)] = differences(b, cols)
-            z0_copy = []
-            for half in range(HALVES):
-                first = work.tile([P, BANK], F32, tag="first")
-                nc.scalar.copy(out=first[:], in_=z0[half][:])
-                z0_copy.append(first)
-            leads = []
-            for half in range(HALVES):
-                cols = slice(half * BANK, (half + 1) * BANK)
-                lead = work.tile([P, BANK], F32, tag="lead")
-                nc.vector.tensor_tensor(out=lead[:], in0=z1[half][:], in1=z0_copy[half][:], op=ALU.subtract)
-                nc.vector.tensor_tensor(out=pair_lse[b][:, cols], in0=z1[half][:], in1=z0_copy[half][:], op=ALU.max)
-                leads.append(lead)
+                h_differences[(b, half)] = differences(b, cols)
+
+        def first_functions(b):
             tanh_pair = work.tile([P, H], F32, tag="tanh_pair")
             for half in range(HALVES):
                 cols = slice(half * BANK, (half + 1) * BANK)
-                nc.scalar.activation(out=tanh_pair[:, cols], in_=leads[half][:], func=ACT.Tanh, scale=0.5)
-            for half in range(HALVES):
-                cols = slice(half * BANK, (half + 1) * BANK)
-                nc.scalar.activation(out=pair_term[b][:, cols], in_=tanh_pair[:, cols], func=ACT.Abs)
+                nc.scalar.activation(out=tanh_pair[:, cols], in_=d1_banks[(b, half)][:], func=ACT.Tanh, scale=0.5)
+                nc.scalar.activation(out=pair_lse[b][:, cols], in_=d1_banks[(b, half)][:], func=ACT.Relu)
             tanh_lead[b] = tanh_pair
+
+        def first_abs(b):
+            nc.scalar.activation(out=pair_term[b][:], in_=tanh_lead[b][:], func=ACT.Abs)
 
         def blend_first_two(b):
             parts = []
@@ -294,57 +293,52 @@ def tile_blocksa_pa_kernel(tc, h, s2t_W1_w, s2t_W1_b, s2t_W_w, out):
                     out=part[:],
                     in0=tanh_lead[b][:, cols],
                     scalar=1.0,
-                    in1=gaps[(b, half)][0][:],
+                    in1=h_differences[(b, half)][0][:],
                     op0=ALU.add,
                     op1=ALU.mult,
                 )
                 parts.append(part)
             for half in range(HALVES):
                 cols = slice(half * BANK, (half + 1) * BANK)
-                nc.vector.tensor_tensor(out=offset[b][:, cols], in0=parts[half][:], in1=gaps[(b, half)][1][:], op=ALU.add)
+                nc.vector.tensor_tensor(out=offset[b][:, cols], in0=parts[half][:], in1=h_differences[(b, half)][1][:], op=ALU.add)
 
-        tanh_third = {}
+        def logarithm(b):
+            nc.scalar.activation(out=pair_term[b][:], in_=pair_term[b][:], func=ACT.Ln, scale=0.5, bias=half_col[:])
+            nc.vector.tensor_tensor(out=pair_lse[b][:], in0=pair_lse[b][:], in1=pair_term[b][:], op=ALU.subtract)
 
-        def third_score(b):
+        def third_lead(b):
             for half in range(HALVES):
                 cols = slice(half * BANK, (half + 1) * BANK)
-                z2 = scores(b, 2, half)
-                lead = work.tile([P, BANK], F32, tag="third_lead")
-                nc.vector.tensor_tensor(out=lead[:], in0=pair_lse[b][:, cols], in1=z2[:], op=ALU.subtract)
-                tanh_last = work.tile([P, BANK], F32, tag="tanh_last", bufs=2 * HALVES)
-                nc.scalar.activation(out=tanh_last[:], in_=lead[:], func=ACT.Tanh, scale=0.5)
-                tanh_third[(b, half)] = tanh_last
+                d2 = score_lead(b, 2, half)
+                nc.vector.tensor_tensor(out=pair_lse[b][:, cols], in0=pair_lse[b][:, cols], in1=d2[:], op=ALU.subtract)
 
         def finish(b):
-            steps = []
+            nc.scalar.activation(out=pair_lse[b][:], in_=pair_lse[b][:], func=ACT.Tanh, scale=0.5)
             for half in range(HALVES):
                 cols = slice(half * BANK, (half + 1) * BANK)
-                step = work.tile([P, BANK], F32, tag="step")
                 nc.vector.scalar_tensor_tensor(
-                    out=step[:],
-                    in0=tanh_third[(b, half)][:],
+                    out=offset[b][:, cols],
+                    in0=pair_lse[b][:, cols],
                     scalar=1.0,
                     in1=offset[b][:, cols],
                     op0=ALU.add,
                     op1=ALU.mult,
                 )
-                steps.append(step)
             for half in range(HALVES):
                 cols = slice(half * BANK, (half + 1) * BANK)
-                result = work.tile([P, BANK], F32, tag="result", bufs=2 * HALVES)
                 nc.vector.scalar_tensor_tensor(
-                    out=result[:],
-                    in0=steps[half][:],
+                    out=offset[b][:, cols],
+                    in0=offset[b][:, cols],
                     scalar=0.5,
                     in1=h_rows[b][:, 2, cols],
                     op0=ALU.mult,
                     op1=ALU.add,
                 )
-                nc.sync.dma_start(out=out_flat[b * P : (b + 1) * P, cols], in_=result[:])
+                nc.sync.dma_start(out=out_flat[b * P : (b + 1) * P, cols], in_=offset[b][:, cols])
 
-        def prepare_weights(rows, codes, scales, r, copies):
+        def prepare_weights(raw_pieces, codes, scales, r, copies):
             cols = slice(r * PIECE, (r + 1) * PIECE)
-            grouped = copy_piece(transpose_piece([rows[r][:, 0, :], rows[r][:, 1, :]]), copies)
+            grouped = copy_piece(transpose_piece([raw_pieces[r][:, 0, :], raw_pieces[r][:, 1, :]]), copies)
             quantise_piece(grouped, codes[:, :, cols], scales[:, :, cols])
 
         transpose_tokens(0)
@@ -368,21 +362,26 @@ def tile_blocksa_pa_kernel(tc, h, s2t_W1_w, s2t_W1_b, s2t_W_w, out):
             hidden_rows(b + 1)
             if b > 0:
                 blend_first_two(b - 1)
+                first_abs(b - 1)
             quantise_tokens(b + 2)
             hidden_codes(b + 1)
-            scores_first_two(b)
-            if b + 3 < token_pieces:
+            first_scores(b)
+            first_functions(b)
+            if b + 3 < TOKEN_PIECES:
                 transpose_tokens(b + 3)
-        hidden_rows(BATCHES + 1)
         blend_first_two(BATCHES - 1)
-        hidden_codes(BATCHES + 1)
 
+        early = BATCHES // 2
+        for b in range(early):
+            logarithm(b)
+        hidden_rows(TOKEN_PIECES - 1)
+        first_abs(BATCHES - 1)
+        hidden_codes(TOKEN_PIECES - 1)
+        third_lead(0)
+        for b in range(early, BATCHES):
+            logarithm(b)
+
+        for b in range(1, BATCHES):
+            third_lead(b)
         for b in range(BATCHES):
-            nc.scalar.activation(out=pair_term[b][:], in_=pair_term[b][:], func=ACT.Ln, scale=0.5, bias=half_col[:])
-            nc.vector.tensor_tensor(out=pair_lse[b][:], in0=pair_lse[b][:], in1=pair_term[b][:], op=ALU.subtract)
-
-        for b in range(BATCHES + 1):
-            if b < BATCHES:
-                third_score(b)
-            if b > 0:
-                finish(b - 1)
+            finish(b)

@@ -24,6 +24,8 @@ WEIGHT_PIECES = H // PIECE
 TOKEN_PIECES = BATCHES * TOKENS * P // PIECE
 ROW_TILES = H // P
 BANK = 512
+SHIFT = 16.0
+LOGBUFS = 2
 HALVES = H // BANK
 RUN = 4
 
@@ -38,7 +40,7 @@ def tile_blocksa_pa_kernel(tc, h, s2t_W1_w, s2t_W1_b, s2t_W_w, out):
     with ExitStack() as stack:
         consts = stack.enter_context(tc.tile_pool(name="consts", bufs=1))
         keep = stack.enter_context(tc.tile_pool(name="keep", bufs=1))
-        raw = stack.enter_context(tc.tile_pool(name="raw", bufs=4))
+        raw = stack.enter_context(tc.tile_pool(name="raw", bufs=8))
         stage = stack.enter_context(tc.tile_pool(name="stage", bufs=3))
         hidden = stack.enter_context(tc.tile_pool(name="hidden", bufs=2))
         work = stack.enter_context(tc.tile_pool(name="work", bufs=2))
@@ -53,13 +55,15 @@ def tile_blocksa_pa_kernel(tc, h, s2t_W1_w, s2t_W1_b, s2t_W_w, out):
             in_=s2t_W1_b.rearrange("(r c) -> r c", r=WEIGHT_PIECES),
         )
         bias = consts.tile([P, ROW_TILES], F32)
-        half_col = consts.tile([P, 1], F32)
-        nc.vector.memset(half_col[:], 0.5)
+        shift_up = consts.tile([P, 1], F32)
+        nc.vector.memset(shift_up[:], SHIFT)
+        shift_down = consts.tile([P, 1], F32)
+        nc.vector.memset(shift_down[:], -SHIFT)
 
         ident = consts.tile([P, P], F32)
         make_identity(nc, ident[:])
         diagonal = {}
-        for value in (0.5, -0.5):
+        for value in (1.0, -1.0):
             scaled = consts.tile([P, P], BF16, name="diagonal%d" % len(diagonal))
             nc.vector.tensor_scalar_mul(out=scaled[:], in0=ident[:], scalar1=value)
             diagonal[value] = scaled
@@ -72,7 +76,7 @@ def tile_blocksa_pa_kernel(tc, h, s2t_W1_w, s2t_W1_b, s2t_W_w, out):
             nc.vector.tensor_copy(out=bias[:], in_=bias_pairs[:].bitcast(BF16))
 
         warm = consts.tile([P, 1], F32)
-        nc.scalar.activation(out=warm[:], in_=half_col[:], func=ACT.Tanh)
+        nc.scalar.activation(out=warm[:], in_=shift_up[:], func=ACT.Sigmoid)
 
         h_rows = []
         for b in range(BATCHES):
@@ -95,7 +99,6 @@ def tile_blocksa_pa_kernel(tc, h, s2t_W1_w, s2t_W1_b, s2t_W_w, out):
             )
             w1_raw.append(rows)
         load_tokens(1, 0, SIDES)
-        load_tokens(2, 0, SIDES)
 
         w2_raw = []
         for r in range(WEIGHT_PIECES):
@@ -106,9 +109,10 @@ def tile_blocksa_pa_kernel(tc, h, s2t_W1_w, s2t_W1_b, s2t_W_w, out):
             )
             w2_raw.append(rows)
 
-        load_tokens(3, 0, SIDES)
-        for b in range(BATCHES):
-            load_tokens(b, SIDES, TOKENS)
+        load_tokens(0, SIDES, TOKENS)
+        load_tokens(1, SIDES, TOKENS)
+        load_tokens(2, 0, TOKENS)
+        load_tokens(3, 0, TOKENS)
 
         w1_codes = keep.tile([P, PASSES, H], U32, align_bytes=64)
         w1_scales = keep.tile([P, PASSES, H], U8, align_bytes=64)
@@ -198,13 +202,14 @@ def tile_blocksa_pa_kernel(tc, h, s2t_W1_w, s2t_W1_b, s2t_W_w, out):
             token_codes[s] = codes
             token_scales[s] = scales
 
-        hidden_rows_of = {}
+        f_rows_of = {}
+        f_banks = {}
+        f_grouped_of = {}
 
-        def hidden_rows(s):
-            f_rows = hidden.tile([P, ROW_TILES, PIECE], BF16, tag="f_rows")
-            hidden_rows_of[s] = f_rows
-            for m in range(ROW_TILES):
+        def hidden_matmuls(s, tiles=range(ROW_TILES)):
+            for m in tiles:
                 bank = psum.tile([P, BANK], F32, tag="bank")
+                f_banks[(s, m)] = bank
                 for g in range(PASSES):
                     nc.tensor.matmul_mx(
                         out=bank[:, 0:PIECE],
@@ -215,30 +220,45 @@ def tile_blocksa_pa_kernel(tc, h, s2t_W1_w, s2t_W1_b, s2t_W_w, out):
                         start=(g == 0),
                         stop=(g == PASSES - 1),
                     )
+
+        def hidden_relus(s, tiles=range(ROW_TILES)):
+            if s not in f_rows_of:
+                f_rows_of[s] = hidden.tile([P, ROW_TILES, PIECE], BF16, tag="f_rows", name="f_rows%d" % s)
+            for m in tiles:
                 nc.scalar.activation(
-                    out=f_rows[:, m, :],
-                    in_=bank[:, 0:PIECE],
+                    out=f_rows_of[s][:, m, :],
+                    in_=f_banks[(s, m)][:, 0:PIECE],
                     func=ACT.Relu,
                     bias=bias[:, m : m + 1],
                     scale=1.0,
                 )
 
-        def hidden_codes(s):
-            f_rows = hidden_rows_of[s]
-            f_grouped = hidden.tile([P, PASSES, PIECE, PACK], BF16, tag="f_grouped", align_bytes=64)
-            for g in range(PASSES):
-                for side in range(SIDES):
-                    cols = slice(side * P, (side + 1) * P)
-                    grouped_side = f_grouped[:, g, cols, :].rearrange("q (c i) t -> q c t i", i=RUN)
-                    rows_side = f_rows[:, g * PACK : (g + 1) * PACK, cols].rearrange("q t (c i) -> q c t i", i=RUN)
-                    if (s, side) in token_0_sides:
-                        nc.vector.tensor_scalar_mul(out=grouped_side, in0=rows_side, scalar1=-1.0)
-                    else:
-                        nc.vector.tensor_copy(out=grouped_side, in_=rows_side)
-            quantise_piece(f_grouped, f_codes[s], f_scales[s])
+        def hidden_rows(s):
+            hidden_matmuls(s)
+            hidden_relus(s)
 
-        def score_lead(b, j, half):
+        def hidden_copies(s, g):
+            if s not in f_grouped_of:
+                f_grouped_of[s] = hidden.tile([P, PASSES, PIECE, PACK], BF16, tag="f_grouped", align_bytes=64, name="f_grouped%d" % s)
+            for side in range(SIDES):
+                cols = slice(side * P, (side + 1) * P)
+                grouped_side = f_grouped_of[s][:, g, cols, :].rearrange("q (c i) t -> q c t i", i=RUN)
+                rows_side = f_rows_of[s][:, g * PACK : (g + 1) * PACK, cols].rearrange("q t (c i) -> q c t i", i=RUN)
+                if (s, side) in token_0_sides:
+                    nc.vector.tensor_scalar_mul(out=grouped_side, in0=rows_side, scalar1=-1.0)
+                else:
+                    nc.vector.tensor_copy(out=grouped_side, in_=rows_side)
+
+        def hidden_codes(s):
+            for g in range(PASSES):
+                hidden_copies(s, g)
+            quantise_piece(f_grouped_of[s], f_codes[s], f_scales[s])
+
+        score_banks = {}
+
+        def scores(b, j, half):
             bank = psum.tile([P, BANK], F32, tag="bank")
+            score_banks[(b, j, half)] = bank
             for token in (j, 0):
                 s, side = piece_of(b, token)
                 for g in range(PASSES):
@@ -251,90 +271,98 @@ def tile_blocksa_pa_kernel(tc, h, s2t_W1_w, s2t_W1_b, s2t_W_w, out):
                         start=(token == j and g == 0),
                         stop=(token == 0 and g == PASSES - 1),
                     )
-            return bank
 
-        tanh_lead = {}
-        h_differences = {}
+        def half_cols(half):
+            return slice(half * BANK, (half + 1) * BANK)
 
-        def differences(b, cols):
-            gap = psum_gap.tile([P, BANK], F32, tag="gap")
-            nc.tensor.matmul(out=gap[:], lhsT=diagonal[0.5][:], rhs=h_rows[b][:, 1, cols], start=True, stop=False)
-            nc.tensor.matmul(out=gap[:], lhsT=diagonal[-0.5][:], rhs=h_rows[b][:, 0, cols], start=False, stop=True)
-            base = work.tile([P, BANK], F32, tag="base", bufs=2 * HALVES)
-            nc.gpsimd.tensor_tensor(out=base[:], in0=h_rows[b][:, 0, cols], in1=h_rows[b][:, 2, cols], op=ALU.subtract)
-            return gap, base
+        gaps = {}
 
-        d1_banks = {}
-
-        def first_scores(b):
+        def gap(b):
             for half in range(HALVES):
-                d1_banks[(b, half)] = score_lead(b, 1, half)
+                cols = half_cols(half)
+                bank = psum_gap.tile([P, BANK], F32, tag="gap")
+                nc.tensor.matmul(out=bank[:], lhsT=diagonal[1.0][:], rhs=h_rows[b][:, 1, cols], start=True, stop=False)
+                nc.tensor.matmul(out=bank[:], lhsT=diagonal[-1.0][:], rhs=h_rows[b][:, 0, cols], start=False, stop=True)
+                gaps[(b, half)] = bank
+
+        def base(b):
             for half in range(HALVES):
-                cols = slice(half * BANK, (half + 1) * BANK)
-                h_differences[(b, half)] = differences(b, cols)
+                cols = half_cols(half)
+                nc.vector.tensor_tensor(out=offset[b][:, cols], in0=h_rows[b][:, 0, cols], in1=h_rows[b][:, 2, cols], op=ALU.subtract)
+
+        def clamp(b, half):
+            nc.scalar.activation(out=pair_lse[b][:, half_cols(half)], in_=score_banks[(b, 1, half)][:], func=ACT.Relu, bias=shift_up[:], scale=1.0)
+
+        def sigma(b, half):
+            cols = half_cols(half)
+            nc.scalar.activation(out=pair_term[b][:, cols], in_=pair_lse[b][:, cols], func=ACT.Sigmoid, bias=shift_down[:], scale=1.0)
 
         def first_functions(b):
-            tanh_pair = work.tile([P, H], F32, tag="tanh_pair")
             for half in range(HALVES):
-                cols = slice(half * BANK, (half + 1) * BANK)
-                nc.scalar.activation(out=tanh_pair[:, cols], in_=d1_banks[(b, half)][:], func=ACT.Tanh, scale=0.5)
-                nc.scalar.activation(out=pair_lse[b][:, cols], in_=d1_banks[(b, half)][:], func=ACT.Relu)
-            tanh_lead[b] = tanh_pair
+                clamp(b, half)
+            for half in range(HALVES):
+                sigma(b, half)
 
-        def first_abs(b):
-            nc.scalar.activation(out=pair_term[b][:], in_=tanh_lead[b][:], func=ACT.Abs)
-
-        def blend_first_two(b):
+        def blend(b):
             parts = []
             for half in range(HALVES):
-                cols = slice(half * BANK, (half + 1) * BANK)
                 part = work.tile([P, BANK], F32, tag="part")
-                nc.vector.scalar_tensor_tensor(
-                    out=part[:],
-                    in0=tanh_lead[b][:, cols],
-                    scalar=1.0,
-                    in1=h_differences[(b, half)][0][:],
-                    op0=ALU.add,
-                    op1=ALU.mult,
-                )
+                nc.vector.tensor_tensor(out=part[:], in0=pair_term[b][:, half_cols(half)], in1=gaps[(b, half)][:], op=ALU.mult)
                 parts.append(part)
             for half in range(HALVES):
-                cols = slice(half * BANK, (half + 1) * BANK)
-                nc.vector.tensor_tensor(out=offset[b][:, cols], in0=parts[half][:], in1=h_differences[(b, half)][1][:], op=ALU.add)
+                cols = half_cols(half)
+                nc.vector.tensor_tensor(out=offset[b][:, cols], in0=parts[half][:], in1=offset[b][:, cols], op=ALU.add)
+
+        logs = {}
 
         def logarithm(b):
-            nc.scalar.activation(out=pair_term[b][:], in_=pair_term[b][:], func=ACT.Ln, scale=0.5, bias=half_col[:])
-            nc.vector.tensor_tensor(out=pair_lse[b][:], in0=pair_lse[b][:], in1=pair_term[b][:], op=ALU.subtract)
-
-        def third_lead(b):
+            logs[b] = work.tile([P, H], F32, tag="log", bufs=LOGBUFS, name="log%d" % b)
             for half in range(HALVES):
-                cols = slice(half * BANK, (half + 1) * BANK)
-                d2 = score_lead(b, 2, half)
-                nc.vector.tensor_tensor(out=pair_lse[b][:, cols], in0=pair_lse[b][:, cols], in1=d2[:], op=ALU.subtract)
+                cols = half_cols(half)
+                nc.scalar.activation(out=logs[b][:, cols], in_=pair_term[b][:, cols], func=ACT.Ln)
+
+        def merge(b):
+            for half in range(HALVES):
+                cols = half_cols(half)
+                nc.vector.tensor_tensor(out=pair_lse[b][:, cols], in0=pair_lse[b][:, cols], in1=logs[b][:, cols], op=ALU.subtract)
+
+        def lead(b):
+            for half in range(HALVES):
+                cols = half_cols(half)
+                nc.vector.tensor_tensor(out=pair_lse[b][:, cols], in0=pair_lse[b][:, cols], in1=score_banks[(b, 2, half)][:], op=ALU.subtract)
+
+        def last_sigma(b):
+            for half in range(HALVES):
+                cols = half_cols(half)
+                nc.scalar.activation(out=pair_lse[b][:, cols], in_=pair_lse[b][:, cols], func=ACT.Sigmoid, bias=shift_down[:], scale=1.0)
 
         def finish(b):
-            nc.scalar.activation(out=pair_lse[b][:], in_=pair_lse[b][:], func=ACT.Tanh, scale=0.5)
             for half in range(HALVES):
-                cols = slice(half * BANK, (half + 1) * BANK)
-                nc.vector.scalar_tensor_tensor(
-                    out=offset[b][:, cols],
-                    in0=pair_lse[b][:, cols],
-                    scalar=1.0,
-                    in1=offset[b][:, cols],
-                    op0=ALU.add,
-                    op1=ALU.mult,
-                )
+                cols = half_cols(half)
+                nc.vector.tensor_tensor(out=offset[b][:, cols], in0=offset[b][:, cols], in1=pair_lse[b][:, cols], op=ALU.mult)
             for half in range(HALVES):
-                cols = slice(half * BANK, (half + 1) * BANK)
-                nc.vector.scalar_tensor_tensor(
-                    out=offset[b][:, cols],
-                    in0=offset[b][:, cols],
-                    scalar=0.5,
-                    in1=h_rows[b][:, 2, cols],
-                    op0=ALU.mult,
-                    op1=ALU.add,
-                )
+                cols = half_cols(half)
+                nc.vector.tensor_tensor(out=offset[b][:, cols], in0=offset[b][:, cols], in1=h_rows[b][:, 2, cols], op=ALU.add)
                 nc.sync.dma_start(out=out_flat[b * P : (b + 1) * P, cols], in_=offset[b][:, cols])
+
+        def d1(b):
+            for half in range(HALVES):
+                scores(b, 1, half)
+
+        def d2(b):
+            for half in range(HALVES):
+                scores(b, 2, half)
+
+        copiers = {"S": nc.scalar.copy, "V": nc.vector.tensor_copy}
+
+        def tok(s, who):
+            copy_tokens(s, [copiers[who[0]], copiers[who[1]]])
+
+        def w1(r, who):
+            prepare_weights(w1_raw, w1_codes, w1_scales, r, [copiers[who[0]], copiers[who[1]]])
+
+        def w2(r, who):
+            prepare_weights(w2_raw, w2_codes, w2_scales, r, [copiers[who[0]], copiers[who[1]]])
 
         def prepare_weights(raw_pieces, codes, scales, r, copies):
             cols = slice(r * PIECE, (r + 1) * PIECE)
@@ -342,46 +370,88 @@ def tile_blocksa_pa_kernel(tc, h, s2t_W1_w, s2t_W1_b, s2t_W_w, out):
             quantise_piece(grouped, codes[:, :, cols], scales[:, :, cols])
 
         transpose_tokens(0)
-        copy_tokens(0, both_engines)
+        tok(0,"SV")
         quantise_tokens(0)
         spread_bias()
-        for r in range(WEIGHT_PIECES):
-            prepare_weights(w1_raw, w1_codes, w1_scales, r, scalar_only)
+        w1(0,"SS")
+        w1(1,"SS")
+        w1(2,"SS")
+        w1(3,"SS")
         transpose_tokens(1)
-        copy_tokens(1, scalar_only)
+        tok(1,"SV")
         quantise_tokens(1)
         hidden_rows(0)
-        prepare_weights(w2_raw, w2_codes, w2_scales, 0, vector_only)
+        w2(0,"SV")
         hidden_codes(0)
-        for r in range(1, WEIGHT_PIECES):
-            prepare_weights(w2_raw, w2_codes, w2_scales, r, scalar_only)
+        w2(1,"SS")
+        w2(2,"SV")
+        w2(3,"SS")
         transpose_tokens(2)
-
-        for b in range(BATCHES):
-            copy_tokens(b + 2, both_engines)
-            hidden_rows(b + 1)
-            if b > 0:
-                blend_first_two(b - 1)
-                first_abs(b - 1)
-            quantise_tokens(b + 2)
-            hidden_codes(b + 1)
-            first_scores(b)
-            first_functions(b)
-            if b + 3 < TOKEN_PIECES:
-                transpose_tokens(b + 3)
-        blend_first_two(BATCHES - 1)
-
-        early = BATCHES // 2
-        for b in range(early):
-            logarithm(b)
-        hidden_rows(TOKEN_PIECES - 1)
-        first_abs(BATCHES - 1)
-        hidden_codes(TOKEN_PIECES - 1)
-        third_lead(0)
-        for b in range(early, BATCHES):
-            logarithm(b)
-
-        for b in range(1, BATCHES):
-            third_lead(b)
-        for b in range(BATCHES):
-            finish(b)
+        base(0)
+        tok(2,"SS")
+        hidden_rows(1)
+        quantise_tokens(2)
+        hidden_codes(1)
+        d1(0)
+        gap(0)
+        first_functions(0)
+        transpose_tokens(4)
+        base(1)
+        tok(4,"SS")
+        hidden_rows(2)
+        blend(0)
+        quantise_tokens(4)
+        hidden_codes(2)
+        d1(1)
+        gap(1)
+        first_functions(1)
+        transpose_tokens(5)
+        base(2)
+        tok(5,"SS")
+        hidden_rows(4)
+        blend(1)
+        quantise_tokens(5)
+        hidden_codes(4)
+        d1(2)
+        gap(2)
+        first_functions(2)
+        transpose_tokens(3)
+        base(3)
+        tok(3,"SV")
+        logarithm(0)
+        hidden_matmuls(5,range(4))
+        d2(0)
+        blend(2)
+        quantise_tokens(3)
+        merge(0)
+        logarithm(1)
+        lead(0)
+        logarithm(2)
+        hidden_relus(5,range(4))
+        hidden_matmuls(5,range(4,8))
+        hidden_relus(5,range(4,8))
+        d2(1)
+        merge(1)
+        hidden_codes(5)
+        lead(1)
+        last_sigma(0)
+        hidden_rows(3)
+        finish(0)
+        last_sigma(1)
+        hidden_codes(3)
+        d2(2)
+        merge(2)
+        lead(2)
+        d1(3)
+        gap(3)
+        first_functions(3)
+        finish(1)
+        last_sigma(2)
+        logarithm(3)
+        blend(3)
+        d2(3)
+        merge(3)
+        lead(3)
+        finish(2)
+        last_sigma(3)
+        finish(3)

@@ -25,7 +25,7 @@ TOKEN_PIECES = BATCHES * TOKENS * P // PIECE
 ROW_TILES = H // P
 BANK = 512
 SHIFT = 16.0
-LOGBUFS = 2
+LOGBUFS = 3
 HALVES = H // BANK
 RUN = 4
 
@@ -41,8 +41,8 @@ def tile_blocksa_pa_kernel(tc, h, s2t_W1_w, s2t_W1_b, s2t_W_w, out):
         consts = stack.enter_context(tc.tile_pool(name="consts", bufs=1))
         keep = stack.enter_context(tc.tile_pool(name="keep", bufs=1))
         raw = stack.enter_context(tc.tile_pool(name="raw", bufs=8))
-        stage = stack.enter_context(tc.tile_pool(name="stage", bufs=3))
-        hidden = stack.enter_context(tc.tile_pool(name="hidden", bufs=2))
+        stage = stack.enter_context(tc.tile_pool(name="stage", bufs=4))
+        hidden = stack.enter_context(tc.tile_pool(name="hidden", bufs=3))
         work = stack.enter_context(tc.tile_pool(name="work", bufs=2))
         psum = stack.enter_context(tc.psum_pool(name="psum", bufs=6))
         psum_gap = stack.enter_context(tc.psum_pool(name="psum_gap", bufs=2))
@@ -50,10 +50,6 @@ def tile_blocksa_pa_kernel(tc, h, s2t_W1_w, s2t_W1_b, s2t_W_w, out):
 
         bias_rows = consts.tile([P, 2 * P], BF16)
         nc.vector.memset(bias_rows[:], 0.0)
-        nc.sync.dma_start(
-            out=bias_rows[0:WEIGHT_PIECES, :],
-            in_=s2t_W1_b.rearrange("(r c) -> r c", r=WEIGHT_PIECES),
-        )
         bias = consts.tile([P, ROW_TILES], F32)
         shift_up = consts.tile([P, 1], F32)
         nc.vector.memset(shift_up[:], SHIFT)
@@ -98,7 +94,12 @@ def tile_blocksa_pa_kernel(tc, h, s2t_W1_w, s2t_W1_b, s2t_W_w, out):
                 in_=s2t_W1_w[r * PIECE : (r + 1) * PIECE, :].rearrange("(q e) k -> q (e k)", e=SIDES),
             )
             w1_raw.append(rows)
+        nc.sync.dma_start(
+            out=bias_rows[0:WEIGHT_PIECES, :],
+            in_=s2t_W1_b.rearrange("(r c) -> r c", r=WEIGHT_PIECES),
+        )
         load_tokens(1, 0, SIDES)
+        load_tokens(2, 0, SIDES)
 
         w2_raw = []
         for r in range(WEIGHT_PIECES):
@@ -109,13 +110,14 @@ def tile_blocksa_pa_kernel(tc, h, s2t_W1_w, s2t_W1_b, s2t_W_w, out):
             )
             w2_raw.append(rows)
 
-        load_tokens(0, SIDES, TOKENS)
-        load_tokens(1, SIDES, TOKENS)
-        load_tokens(2, 0, TOKENS)
-        load_tokens(3, 0, TOKENS)
+        for b in range(SIDES):
+            load_tokens(b, SIDES, TOKENS)
+        load_tokens(3, 0, SIDES)
+        for b in range(SIDES, BATCHES):
+            load_tokens(b, SIDES, TOKENS)
 
-        w1_codes = keep.tile([P, PASSES, H], U32, align_bytes=64)
-        w1_scales = keep.tile([P, PASSES, H], U8, align_bytes=64)
+        w1_codes = keep.tile([P, WEIGHT_PIECES, PASSES, PIECE], U32, align_bytes=64)
+        w1_scales = keep.tile([P, WEIGHT_PIECES, PASSES, PIECE], U8, align_bytes=64)
         w2_codes = keep.tile([P, PASSES, H], U32, align_bytes=64)
         w2_scales = keep.tile([P, PASSES, H], U8, align_bytes=64)
         f_codes = []
@@ -172,6 +174,13 @@ def tile_blocksa_pa_kernel(tc, h, s2t_W1_w, s2t_W1_b, s2t_W_w, out):
                 )
             return grouped
 
+        def quantise_whole(grouped, codes, scales):
+            nc.vector.quantize_mx(
+                out=codes.rearrange("q g c -> q (g c)").bitcast(FP8X4),
+                scales=scales.rearrange("q g c -> q (g c)"),
+                in_=grouped[:].rearrange("q g c t -> q (g c t)"),
+            )
+
         def quantise_piece(grouped, codes, scales):
             for g in range(PASSES):
                 nc.vector.quantize_mx(
@@ -198,7 +207,7 @@ def tile_blocksa_pa_kernel(tc, h, s2t_W1_w, s2t_W1_b, s2t_W_w, out):
         def quantise_tokens(s):
             codes = stage.tile([P, PASSES, PIECE], U32, tag="token_codes", align_bytes=64)
             scales = stage.tile([P, PASSES, PIECE], U8, tag="token_scales", align_bytes=64)
-            quantise_piece(token_grouped[s], codes, scales)
+            quantise_whole(token_grouped[s], codes[:], scales[:])
             token_codes[s] = codes
             token_scales[s] = scales
 
@@ -208,13 +217,15 @@ def tile_blocksa_pa_kernel(tc, h, s2t_W1_w, s2t_W1_b, s2t_W_w, out):
 
         def hidden_matmuls(s, tiles=range(ROW_TILES)):
             for m in tiles:
-                bank = psum.tile([P, BANK], F32, tag="bank")
-                f_banks[(s, m)] = bank
+                if m % 2 == 0:
+                    bank = psum.tile([P, 2, PIECE], F32, tag="bank", name="f_bank")
+                    f_banks[(s, m // 2)] = bank
+                bank = f_banks[(s, m // 2)]
                 for g in range(PASSES):
                     nc.tensor.matmul_mx(
-                        out=bank[:, 0:PIECE],
-                        lhsT=w1_codes[:, g, m * P : (m + 1) * P].bitcast(FP8X4),
-                        lhsT_scale=w1_scales[:, g, m * P : (m + 1) * P],
+                        out=bank[:, m % 2, :],
+                        lhsT=w1_codes[:, m // 2, g, (m % 2) * P : (m % 2 + 1) * P].bitcast(FP8X4),
+                        lhsT_scale=w1_scales[:, m // 2, g, (m % 2) * P : (m % 2 + 1) * P],
                         rhs=token_codes[s][:, g, :].bitcast(FP8X4),
                         rhs_scale=token_scales[s][:, g, :],
                         start=(g == 0),
@@ -224,10 +235,10 @@ def tile_blocksa_pa_kernel(tc, h, s2t_W1_w, s2t_W1_b, s2t_W_w, out):
         def hidden_relus(s, tiles=range(ROW_TILES)):
             if s not in f_rows_of:
                 f_rows_of[s] = hidden.tile([P, ROW_TILES, PIECE], BF16, tag="f_rows", name="f_rows%d" % s)
-            for m in tiles:
+            for m in [m + 1 - 2 * (m % 2) for m in tiles]:
                 nc.scalar.activation(
                     out=f_rows_of[s][:, m, :],
-                    in_=f_banks[(s, m)][:, 0:PIECE],
+                    in_=f_banks[(s, m // 2)][:, m % 2, :],
                     func=ACT.Relu,
                     bias=bias[:, m : m + 1],
                     scale=1.0,
@@ -240,8 +251,8 @@ def tile_blocksa_pa_kernel(tc, h, s2t_W1_w, s2t_W1_b, s2t_W_w, out):
         def hidden_copies(s, g):
             if s not in f_grouped_of:
                 f_grouped_of[s] = hidden.tile([P, PASSES, PIECE, PACK], BF16, tag="f_grouped", align_bytes=64, name="f_grouped%d" % s)
-            for side in range(SIDES):
-                cols = slice(side * P, (side + 1) * P)
+            for side in range(SIDES) if s < BATCHES else [None]:
+                cols = slice(0, PIECE) if side is None else slice(side * P, (side + 1) * P)
                 grouped_side = f_grouped_of[s][:, g, cols, :].rearrange("q (c i) t -> q c t i", i=RUN)
                 rows_side = f_rows_of[s][:, g * PACK : (g + 1) * PACK, cols].rearrange("q t (c i) -> q c t i", i=RUN)
                 if (s, side) in token_0_sides:
@@ -252,7 +263,10 @@ def tile_blocksa_pa_kernel(tc, h, s2t_W1_w, s2t_W1_b, s2t_W_w, out):
         def hidden_codes(s):
             for g in range(PASSES):
                 hidden_copies(s, g)
-            quantise_piece(f_grouped_of[s], f_codes[s], f_scales[s])
+            quantise_f(s)
+
+        def quantise_f(s):
+            quantise_whole(f_grouped_of[s], f_codes[s][:], f_scales[s][:])
 
         score_banks = {}
 
@@ -286,9 +300,7 @@ def tile_blocksa_pa_kernel(tc, h, s2t_W1_w, s2t_W1_b, s2t_W_w, out):
                 gaps[(b, half)] = bank
 
         def base(b):
-            for half in range(HALVES):
-                cols = half_cols(half)
-                nc.vector.tensor_tensor(out=offset[b][:, cols], in0=h_rows[b][:, 0, cols], in1=h_rows[b][:, 2, cols], op=ALU.subtract)
+            nc.vector.tensor_tensor(out=offset[b][:], in0=h_rows[b][:, 0, :], in1=h_rows[b][:, 2, :], op=ALU.subtract)
 
         def clamp(b, half):
             nc.scalar.activation(out=pair_lse[b][:, half_cols(half)], in_=score_banks[(b, 1, half)][:], func=ACT.Relu, bias=shift_up[:], scale=1.0)
@@ -345,6 +357,27 @@ def tile_blocksa_pa_kernel(tc, h, s2t_W1_w, s2t_W1_b, s2t_W_w, out):
                 nc.vector.tensor_tensor(out=offset[b][:, cols], in0=offset[b][:, cols], in1=h_rows[b][:, 2, cols], op=ALU.add)
                 nc.sync.dma_start(out=out_flat[b * P : (b + 1) * P, cols], in_=offset[b][:, cols])
 
+        sum_banks = {}
+
+        def weigh(b):
+            for half in range(HALVES):
+                cols = half_cols(half)
+                nc.vector.tensor_tensor(out=offset[b][:, cols], in0=offset[b][:, cols], in1=pair_lse[b][:, cols], op=ALU.mult)
+
+        def sum_tensor(b):
+            for half in range(HALVES):
+                cols = half_cols(half)
+                bank = psum.tile([P, BANK], F32, tag="bank", name="sum_bank")
+                nc.tensor.matmul(out=bank[:], lhsT=diagonal[1.0][:], rhs=h_rows[b][:, 2, cols], start=True, stop=False)
+                nc.tensor.matmul(out=bank[:], lhsT=ident[:], rhs=offset[b][:, cols], start=False, stop=True)
+                sum_banks[(b, half)] = bank
+
+        def store_sum(b):
+            for half in range(HALVES):
+                cols = half_cols(half)
+                nc.scalar.copy(out=pair_term[b][:, cols], in_=sum_banks[(b, half)][:])
+                nc.sync.dma_start(out=out_flat[b * P : (b + 1) * P, cols], in_=pair_term[b][:, cols])
+
         def d1(b):
             for half in range(HALVES):
                 scores(b, 1, half)
@@ -361,96 +394,173 @@ def tile_blocksa_pa_kernel(tc, h, s2t_W1_w, s2t_W1_b, s2t_W_w, out):
         def w1(r, who):
             prepare_weights(w1_raw, w1_codes, w1_scales, r, [copiers[who[0]], copiers[who[1]]])
 
-        def w2(r, who):
-            prepare_weights(w2_raw, w2_codes, w2_scales, r, [copiers[who[0]], copiers[who[1]]])
+        w2_banks = {}
+        w2_grouped = {}
+
+        def w2_transposes(r):
+            w2_banks[r] = transpose_piece([w2_raw[r][:, 0, :], w2_raw[r][:, 1, :]])
+
+        def w2_copies(r, who):
+            w2_grouped[r] = copy_piece(w2_banks[r], [copiers[who[0]], copiers[who[1]]])
+
+        def w2_quantise(r):
+            cols = slice(r * PIECE, (r + 1) * PIECE)
+            quantise_piece(w2_grouped[r], w2_codes[:, :, cols], w2_scales[:, :, cols])
+
+        w1_banks = {}
+        w1_grouped = {}
+
+        def w1_transposes(r):
+            w1_banks[r] = transpose_piece([w1_raw[r][:, 0, :], w1_raw[r][:, 1, :]])
+
+        def w1_copies(r, who):
+            w1_grouped[r] = copy_piece(w1_banks[r], [copiers[who[0]], copiers[who[1]]])
+
+        def w1_quantise(r):
+            quantise_whole(w1_grouped[r], w1_codes[:, r], w1_scales[:, r])
+
+        def first_clamp(b):
+            for half in range(HALVES):
+                clamp(b, half)
+
+        def first_sigma(b):
+            nc.scalar.activation(out=pair_term[b][:], in_=pair_lse[b][:], func=ACT.Sigmoid, bias=shift_down[:], scale=1.0)
+
+        def log_wide(b):
+            logs[b] = work.tile([P, H], F32, tag="log", bufs=LOGBUFS, name="log%d" % b)
+            nc.scalar.activation(out=logs[b][:], in_=pair_term[b][:], func=ACT.Ln)
+
+        def merge_wide(b):
+            nc.vector.tensor_tensor(out=pair_lse[b][:], in0=pair_lse[b][:], in1=logs[b][:], op=ALU.subtract)
 
         def prepare_weights(raw_pieces, codes, scales, r, copies):
-            cols = slice(r * PIECE, (r + 1) * PIECE)
             grouped = copy_piece(transpose_piece([raw_pieces[r][:, 0, :], raw_pieces[r][:, 1, :]]), copies)
-            quantise_piece(grouped, codes[:, :, cols], scales[:, :, cols])
+            if codes is w1_codes:
+                quantise_whole(grouped, codes[:, r], scales[:, r])
+            else:
+                cols = slice(r * PIECE, (r + 1) * PIECE)
+                quantise_piece(grouped, codes[:, :, cols], scales[:, :, cols])
 
         transpose_tokens(0)
         tok(0,"SV")
+        w1_transposes(0)
+        w1_copies(0,"VS")
         quantise_tokens(0)
+        w1_transposes(1)
+        w1_copies(1,"VS")
+        w1_transposes(2)
+        w1_quantise(0)
+        w1_copies(2,"SS")
+        w1_quantise(1)
+        w1_transposes(3)
         spread_bias()
-        w1(0,"SS")
-        w1(1,"SS")
-        w1(2,"SS")
-        w1(3,"SS")
+        gap(0)
+        w1_copies(3,"VS")
+        w1_quantise(2)
         transpose_tokens(1)
         tok(1,"SV")
+        w1_quantise(3)
         quantise_tokens(1)
-        hidden_rows(0)
-        w2(0,"SV")
-        hidden_codes(0)
-        w2(1,"SS")
-        w2(2,"SV")
-        w2(3,"SS")
+        hidden_matmuls(0)
         transpose_tokens(2)
-        base(0)
-        tok(2,"SS")
-        hidden_rows(1)
+        hidden_relus(0)
+        tok(2,"SV")
+
+        w2_transposes(0)
+        w2_copies(0,"SS")
+        hidden_copies(0,0)
+        hidden_copies(0,1)
         quantise_tokens(2)
-        hidden_codes(1)
-        d1(0)
-        gap(0)
-        first_functions(0)
-        transpose_tokens(4)
+        hidden_matmuls(1)
+        quantise_f(0)
+        w2_quantise(0)
+        w2_transposes(1)
+        hidden_relus(1)
+        w2_copies(1,"SS")
+        base(0)
+        w2_transposes(2)
+        w2_copies(2,"VS")
+        w2_quantise(1)
+        hidden_copies(1,0)
+        hidden_copies(1,1)
+        w2_quantise(2)
+        quantise_f(1)
+        hidden_matmuls(2)
+        w2_transposes(3)
+        hidden_relus(2)
+        w2_copies(3,"VS")
         base(1)
+        w2_quantise(3)
+
+        transpose_tokens(4)
         tok(4,"SS")
-        hidden_rows(2)
-        blend(0)
-        quantise_tokens(4)
-        hidden_codes(2)
-        d1(1)
-        gap(1)
-        first_functions(1)
         transpose_tokens(5)
-        base(2)
         tok(5,"SS")
-        hidden_rows(4)
-        blend(1)
+        hidden_copies(2,0)
+        hidden_copies(2,1)
+        quantise_tokens(4)
+        quantise_f(2)
+        base(2)
         quantise_tokens(5)
-        hidden_codes(4)
-        d1(2)
-        gap(2)
-        first_functions(2)
-        transpose_tokens(3)
+
+        d1(0)
+        first_clamp(0)
+        first_sigma(0)
+        hidden_matmuls(4)
+        d1(1)
+        hidden_relus(4)
+        first_clamp(1)
+        blend(0)
         base(3)
-        tok(3,"SV")
-        logarithm(0)
-        hidden_matmuls(5,range(4))
-        d2(0)
-        blend(2)
+        first_sigma(1)
+        gap(1)
+        transpose_tokens(3)
+        tok(3,"SS")
+        hidden_copies(4,0)
+        hidden_copies(4,1)
         quantise_tokens(3)
-        merge(0)
-        logarithm(1)
+        quantise_f(4)
+        hidden_matmuls(5)
+        blend(1)
+        d1(2)
+        hidden_relus(5)
+        first_clamp(2)
+        first_sigma(2)
+        gap(2)
+        hidden_copies(5,0)
+        hidden_copies(5,1)
+        hidden_matmuls(3)
+        hidden_relus(3)
+        blend(2)
+        quantise_f(5)
+        log_wide(0)
+        log_wide(1)
+        log_wide(2)
+        hidden_copies(3,0)
+        hidden_copies(3,1)
+        d2(0)
+        quantise_f(3)
+        merge_wide(0)
+        d1(3)
+        merge_wide(1)
         lead(0)
-        logarithm(2)
-        hidden_relus(5,range(4))
-        hidden_matmuls(5,range(4,8))
-        hidden_relus(5,range(4,8))
+        first_clamp(3)
         d2(1)
-        merge(1)
-        hidden_codes(5)
+        merge_wide(2)
         lead(1)
         last_sigma(0)
-        hidden_rows(3)
+        first_sigma(3)
+        gap(3)
+        d2(2)
         finish(0)
         last_sigma(1)
-        hidden_codes(3)
-        d2(2)
-        merge(2)
-        lead(2)
-        d1(3)
-        gap(3)
-        first_functions(3)
-        finish(1)
-        last_sigma(2)
-        logarithm(3)
         blend(3)
+        lead(2)
+        log_wide(3)
         d2(3)
+        finish(1)
         merge(3)
+        last_sigma(2)
         lead(3)
         finish(2)
         last_sigma(3)

@@ -25,7 +25,7 @@ TOKEN_PIECES = BATCHES * TOKENS * P // PIECE
 ROW_TILES = H // P
 BANK = 512
 SHIFT = 16.0
-LOGBUFS = 3
+LOGBUFS = 4
 HALVES = H // BANK
 RUN = 4
 
@@ -297,7 +297,13 @@ def tile_blocksa_pa_kernel(tc, h, s2t_W1_w, s2t_W1_b, s2t_W_w, out):
                 bank = psum_gap.tile([P, BANK], F32, tag="gap")
                 nc.tensor.matmul(out=bank[:], lhsT=diagonal[1.0][:], rhs=h_rows[b][:, 1, cols], start=True, stop=False)
                 nc.tensor.matmul(out=bank[:], lhsT=diagonal[-1.0][:], rhs=h_rows[b][:, 0, cols], start=False, stop=True)
-                gaps[(b, half)] = bank
+                gaps[(b, half)] = bank[:]
+
+        def gap_vector(b):
+            tile_ = work.tile([P, H], F32, tag="gapv", name="gapv%d" % b)
+            nc.vector.tensor_tensor(out=tile_[:], in0=h_rows[b][:, 1, :], in1=h_rows[b][:, 0, :], op=ALU.subtract)
+            for half in range(HALVES):
+                gaps[(b, half)] = tile_[:, half_cols(half)]
 
         def base(b):
             nc.vector.tensor_tensor(out=offset[b][:], in0=h_rows[b][:, 0, :], in1=h_rows[b][:, 2, :], op=ALU.subtract)
@@ -319,7 +325,7 @@ def tile_blocksa_pa_kernel(tc, h, s2t_W1_w, s2t_W1_b, s2t_W_w, out):
             parts = []
             for half in range(HALVES):
                 part = work.tile([P, BANK], F32, tag="part")
-                nc.vector.tensor_tensor(out=part[:], in0=pair_term[b][:, half_cols(half)], in1=gaps[(b, half)][:], op=ALU.mult)
+                nc.vector.tensor_tensor(out=part[:], in0=pair_term[b][:, half_cols(half)], in1=gaps[(b, half)], op=ALU.mult)
                 parts.append(part)
             for half in range(HALVES):
                 cols = half_cols(half)
@@ -443,6 +449,7 @@ def tile_blocksa_pa_kernel(tc, h, s2t_W1_w, s2t_W1_b, s2t_W_w, out):
 
         transpose_tokens(0)
         tok(0,"SV")
+        gap(0)
         w1_transposes(0)
         w1_copies(0,"VS")
         quantise_tokens(0)
@@ -454,7 +461,6 @@ def tile_blocksa_pa_kernel(tc, h, s2t_W1_w, s2t_W1_b, s2t_W_w, out):
         w1_quantise(1)
         w1_transposes(3)
         spread_bias()
-        gap(0)
         w1_copies(3,"VS")
         w1_quantise(2)
         transpose_tokens(1)
@@ -513,7 +519,7 @@ def tile_blocksa_pa_kernel(tc, h, s2t_W1_w, s2t_W1_b, s2t_W_w, out):
         blend(0)
         base(3)
         first_sigma(1)
-        gap(1)
+        gap_vector(1)
         transpose_tokens(3)
         tok(3,"SS")
         hidden_copies(4,0)
@@ -552,16 +558,20 @@ def tile_blocksa_pa_kernel(tc, h, s2t_W1_w, s2t_W1_b, s2t_W_w, out):
         first_sigma(3)
         gap(3)
         d2(2)
-        finish(0)
+        weigh(0)
         last_sigma(1)
         blend(3)
+        sum_tensor(0)
         lead(2)
         log_wide(3)
         d2(3)
-        finish(1)
+        weigh(1)
         merge(3)
+        store_sum(0)
+        sum_tensor(1)
         last_sigma(2)
         lead(3)
         finish(2)
         last_sigma(3)
+        store_sum(1)
         finish(3)

@@ -25,7 +25,8 @@ TOKEN_PIECES = BATCHES * TOKENS * P // PIECE
 ROW_TILES = H // P
 BANK = 512
 SHIFT = 16.0
-LOGBUFS = 4
+LOGBUFS = 3
+WARM = 6
 HALVES = H // BANK
 RUN = 4
 
@@ -48,6 +49,8 @@ def tile_blocksa_pa_kernel(tc, h, s2t_W1_w, s2t_W1_b, s2t_W_w, out):
         psum_gap = stack.enter_context(tc.psum_pool(name="psum_gap", bufs=2))
         stack.enter_context(tc.manual_schedule())
 
+        zeros = consts.tile([P, BANK], BF16)
+        nc.vector.memset(zeros[:], 0.0)
         bias_rows = consts.tile([P, 2 * P], BF16)
         nc.vector.memset(bias_rows[:], 0.0)
         bias = consts.tile([P, ROW_TILES], F32)
@@ -71,6 +74,9 @@ def tile_blocksa_pa_kernel(tc, h, s2t_W1_w, s2t_W1_b, s2t_W_w, out):
             nc.vector.tensor_copy(out=bias_pairs[:], in_=bias_bank[:, 0:WEIGHT_PIECES])
             nc.vector.tensor_copy(out=bias[:], in_=bias_pairs[:].bitcast(BF16))
 
+        warm_bank = psum_gap.tile([P, BANK], F32, tag="gap", name="warm_bank")
+        for i in range(WARM):
+            nc.tensor.matmul(out=warm_bank[:], lhsT=zeros[:, 0:P], rhs=zeros[:], start=True, stop=True)
         warm = consts.tile([P, 1], F32)
         nc.scalar.activation(out=warm[:], in_=shift_up[:], func=ACT.Sigmoid)
 
@@ -291,8 +297,8 @@ def tile_blocksa_pa_kernel(tc, h, s2t_W1_w, s2t_W1_b, s2t_W_w, out):
 
         gaps = {}
 
-        def gap(b):
-            for half in range(HALVES):
+        def gap(b, halves=range(HALVES)):
+            for half in halves:
                 cols = half_cols(half)
                 bank = psum_gap.tile([P, BANK], F32, tag="gap")
                 nc.tensor.matmul(out=bank[:], lhsT=diagonal[1.0][:], rhs=h_rows[b][:, 1, cols], start=True, stop=False)
@@ -449,13 +455,14 @@ def tile_blocksa_pa_kernel(tc, h, s2t_W1_w, s2t_W1_b, s2t_W_w, out):
 
         transpose_tokens(0)
         tok(0,"SV")
-        gap(0)
         w1_transposes(0)
+        gap(0,[0])
         w1_copies(0,"VS")
         quantise_tokens(0)
         w1_transposes(1)
         w1_copies(1,"VS")
         w1_transposes(2)
+        gap(0,[1])
         w1_quantise(0)
         w1_copies(2,"SS")
         w1_quantise(1)
@@ -464,8 +471,8 @@ def tile_blocksa_pa_kernel(tc, h, s2t_W1_w, s2t_W1_b, s2t_W_w, out):
         w1_copies(3,"VS")
         w1_quantise(2)
         transpose_tokens(1)
-        tok(1,"SV")
         w1_quantise(3)
+        tok(1,"SV")
         quantise_tokens(1)
         hidden_matmuls(0)
         transpose_tokens(2)
@@ -503,25 +510,25 @@ def tile_blocksa_pa_kernel(tc, h, s2t_W1_w, s2t_W1_b, s2t_W_w, out):
         transpose_tokens(5)
         tok(5,"SS")
         hidden_copies(2,0)
-        hidden_copies(2,1)
         quantise_tokens(4)
-        quantise_f(2)
-        base(2)
         quantise_tokens(5)
+        hidden_copies(2,1)
 
         d1(0)
         first_clamp(0)
         first_sigma(0)
         hidden_matmuls(4)
         d1(1)
+        gap_vector(1)
+        quantise_f(2)
         hidden_relus(4)
         first_clamp(1)
+        base(2)
         blend(0)
         base(3)
-        first_sigma(1)
-        gap_vector(1)
         transpose_tokens(3)
         tok(3,"SS")
+        first_sigma(1)
         hidden_copies(4,0)
         hidden_copies(4,1)
         quantise_tokens(3)
@@ -539,6 +546,7 @@ def tile_blocksa_pa_kernel(tc, h, s2t_W1_w, s2t_W1_b, s2t_W_w, out):
         hidden_relus(3)
         blend(2)
         quantise_f(5)
+
         log_wide(0)
         log_wide(1)
         log_wide(2)
@@ -547,9 +555,9 @@ def tile_blocksa_pa_kernel(tc, h, s2t_W1_w, s2t_W1_b, s2t_W_w, out):
         d2(0)
         quantise_f(3)
         merge_wide(0)
+        lead(0)
         d1(3)
         merge_wide(1)
-        lead(0)
         first_clamp(3)
         d2(1)
         merge_wide(2)
@@ -560,16 +568,16 @@ def tile_blocksa_pa_kernel(tc, h, s2t_W1_w, s2t_W1_b, s2t_W_w, out):
         d2(2)
         weigh(0)
         last_sigma(1)
+        lead(2)
         blend(3)
         sum_tensor(0)
-        lead(2)
         log_wide(3)
+        last_sigma(2)
         d2(3)
         weigh(1)
         merge(3)
         store_sum(0)
         sum_tensor(1)
-        last_sigma(2)
         lead(3)
         finish(2)
         last_sigma(3)

@@ -25,7 +25,7 @@ TOKEN_PIECES = BATCHES * TOKENS * P // PIECE
 ROW_TILES = H // P
 BANK = 512
 SHIFT = 16.0
-LOGBUFS = 3
+LOGBUFS = 4
 WARM = 6
 HALVES = H // BANK
 RUN = 4
@@ -477,11 +477,11 @@ def tile_blocksa_pa_kernel(tc, h, s2t_W1_w, s2t_W1_b, s2t_W_w, out):
         hidden_matmuls(0)
         transpose_tokens(2)
         hidden_relus(0)
+        hidden_copies(0,0)
         tok(2,"SV")
 
         w2_transposes(0)
         w2_copies(0,"SS")
-        hidden_copies(0,0)
         hidden_copies(0,1)
         quantise_tokens(2)
         hidden_matmuls(1)
@@ -507,79 +507,81 @@ def tile_blocksa_pa_kernel(tc, h, s2t_W1_w, s2t_W1_b, s2t_W_w, out):
 
         transpose_tokens(4)
         tok(4,"SS")
-        transpose_tokens(5)
-        tok(5,"SS")
-        hidden_copies(2,0)
+        transpose_tokens(3)
+        tok(3,"SS")
         quantise_tokens(4)
-        quantise_tokens(5)
+        quantise_tokens(3)
+        hidden_copies(2,0)
         hidden_copies(2,1)
+        base(2)
 
         d1(0)
         first_clamp(0)
         first_sigma(0)
         hidden_matmuls(4)
         d1(1)
-        gap_vector(1)
         quantise_f(2)
         hidden_relus(4)
         first_clamp(1)
-        base(2)
         blend(0)
+        gap_vector(1)
         base(3)
-        transpose_tokens(3)
-        tok(3,"SS")
+        transpose_tokens(5)
+        tok(5,"SS")
         first_sigma(1)
         hidden_copies(4,0)
         hidden_copies(4,1)
-        quantise_tokens(3)
-        quantise_f(4)
-        hidden_matmuls(5)
+        quantise_tokens(5)
+        hidden_matmuls(3)
         blend(1)
         d1(2)
-        hidden_relus(5)
+        hidden_relus(3)
         first_clamp(2)
         first_sigma(2)
         gap(2)
+        hidden_copies(3,0)
+        hidden_copies(3,1)
+        quantise_f(3)
+        quantise_f(4)
+        hidden_matmuls(5)
+        d1(3)
+        gap(3)
+        hidden_relus(5)
+        blend(2)
+        first_clamp(3)
+        first_sigma(3)
         hidden_copies(5,0)
         hidden_copies(5,1)
-        hidden_matmuls(3)
-        hidden_relus(3)
-        blend(2)
+        d2(0)
         quantise_f(5)
 
         log_wide(0)
         log_wide(1)
+        blend(3)
         log_wide(2)
-        hidden_copies(3,0)
-        hidden_copies(3,1)
-        d2(0)
-        quantise_f(3)
+        log_wide(3)
         merge_wide(0)
-        lead(0)
-        d1(3)
         merge_wide(1)
-        first_clamp(3)
+        lead(0)
         d2(1)
+        d2(2)
+        d2(3)
         merge_wide(2)
         lead(1)
         last_sigma(0)
-        first_sigma(3)
-        gap(3)
-        d2(2)
-        weigh(0)
         last_sigma(1)
+        weigh(0)
+        merge_wide(3)
         lead(2)
-        blend(3)
-        sum_tensor(0)
-        log_wide(3)
         last_sigma(2)
-        d2(3)
+        sum_tensor(0)
         weigh(1)
-        merge(3)
-        store_sum(0)
-        sum_tensor(1)
         lead(3)
-        finish(2)
+        sum_tensor(1)
+        store_sum(0)
         last_sigma(3)
+        weigh(2)
         store_sum(1)
+        sum_tensor(2)
         finish(3)
+        store_sum(2)

@@ -26,6 +26,7 @@ ROW_TILES = H // P
 BANK = 512
 SHIFT = 16.0
 LOGBUFS = 4
+GBUFS = 1
 WARM = 6
 HALVES = H // BANK
 RUN = 4
@@ -49,8 +50,6 @@ def tile_blocksa_pa_kernel(tc, h, s2t_W1_w, s2t_W1_b, s2t_W_w, out):
         psum_gap = stack.enter_context(tc.psum_pool(name="psum_gap", bufs=2))
         stack.enter_context(tc.manual_schedule())
 
-        zeros = consts.tile([P, BANK], BF16)
-        nc.vector.memset(zeros[:], 0.0)
         bias_rows = consts.tile([P, 2 * P], BF16)
         nc.vector.memset(bias_rows[:], 0.0)
         bias = consts.tile([P, ROW_TILES], F32)
@@ -74,6 +73,8 @@ def tile_blocksa_pa_kernel(tc, h, s2t_W1_w, s2t_W1_b, s2t_W_w, out):
             nc.vector.tensor_copy(out=bias_pairs[:], in_=bias_bank[:, 0:WEIGHT_PIECES])
             nc.vector.tensor_copy(out=bias[:], in_=bias_pairs[:].bitcast(BF16))
 
+        zeros = consts.tile([P, BANK], BF16)
+        nc.vector.memset(zeros[:], 0.0)
         warm_bank = psum_gap.tile([P, BANK], F32, tag="gap", name="warm_bank")
         for i in range(WARM):
             nc.tensor.matmul(out=warm_bank[:], lhsT=zeros[:, 0:P], rhs=zeros[:], start=True, stop=True)
@@ -105,6 +106,7 @@ def tile_blocksa_pa_kernel(tc, h, s2t_W1_w, s2t_W1_b, s2t_W_w, out):
             in_=s2t_W1_b.rearrange("(r c) -> r c", r=WEIGHT_PIECES),
         )
         load_tokens(1, 0, SIDES)
+        load_tokens(0, SIDES, TOKENS)
         load_tokens(2, 0, SIDES)
 
         w2_raw = []
@@ -116,9 +118,8 @@ def tile_blocksa_pa_kernel(tc, h, s2t_W1_w, s2t_W1_b, s2t_W_w, out):
             )
             w2_raw.append(rows)
 
-        for b in range(SIDES):
-            load_tokens(b, SIDES, TOKENS)
         load_tokens(3, 0, SIDES)
+        load_tokens(1, SIDES, TOKENS)
         for b in range(SIDES, BATCHES):
             load_tokens(b, SIDES, TOKENS)
 
@@ -296,6 +297,7 @@ def tile_blocksa_pa_kernel(tc, h, s2t_W1_w, s2t_W1_b, s2t_W_w, out):
             return slice(half * BANK, (half + 1) * BANK)
 
         gaps = {}
+        bases = {}
 
         def gap(b, halves=range(HALVES)):
             for half in halves:
@@ -305,14 +307,62 @@ def tile_blocksa_pa_kernel(tc, h, s2t_W1_w, s2t_W1_b, s2t_W_w, out):
                 nc.tensor.matmul(out=bank[:], lhsT=diagonal[-1.0][:], rhs=h_rows[b][:, 0, cols], start=False, stop=True)
                 gaps[(b, half)] = bank[:]
 
+        def gap_term(b, half, token):
+            cols = half_cols(half)
+            if token == 1:
+                gaps[(b, half)] = psum_gap.tile([P, BANK], F32, tag="gap", name="gap_bank")[:]
+            nc.tensor.matmul(out=gaps[(b, half)], lhsT=diagonal[1.0 if token == 1 else -1.0][:], rhs=h_rows[b][:, token, cols], start=(token == 1), stop=(token == 0))
+
         def gap_vector(b):
-            tile_ = work.tile([P, H], F32, tag="gapv", name="gapv%d" % b)
+            tile_ = work.tile([P, H], F32, tag="gapv", bufs=1, name="gapv%d" % b)
             nc.vector.tensor_tensor(out=tile_[:], in0=h_rows[b][:, 1, :], in1=h_rows[b][:, 0, :], op=ALU.subtract)
             for half in range(HALVES):
                 gaps[(b, half)] = tile_[:, half_cols(half)]
 
-        def base(b):
-            nc.vector.tensor_tensor(out=offset[b][:], in0=h_rows[b][:, 0, :], in1=h_rows[b][:, 2, :], op=ALU.subtract)
+        def base_vector(b, halves=range(HALVES)):
+            if len(halves) == HALVES:
+                nc.vector.tensor_tensor(out=offset[b][:], in0=h_rows[b][:, 0, :], in1=h_rows[b][:, 2, :], op=ALU.subtract)
+            for half in halves:
+                cols = half_cols(half)
+                bases[(b, half)] = offset[b][:, cols]
+                if len(halves) < HALVES:
+                    nc.vector.tensor_tensor(out=bases[(b, half)], in0=h_rows[b][:, 0, cols], in1=h_rows[b][:, 2, cols], op=ALU.subtract)
+
+        def base_gpsimd(b):
+            tile_ = work.tile([P, H], F32, tag="baseg", bufs=GBUFS, name="baseg%d" % b)
+            for half in range(HALVES):
+                cols = half_cols(half)
+                nc.gpsimd.tensor_tensor(out=tile_[:, cols], in0=h_rows[b][:, 0, cols], in1=h_rows[b][:, 2, cols], op=ALU.subtract)
+                bases[(b, half)] = tile_[:, cols]
+
+        def gap_gpsimd(b):
+            tile_ = work.tile([P, H], F32, tag="gapg", bufs=GBUFS, name="gapg%d" % b)
+            for half in range(HALVES):
+                cols = half_cols(half)
+                nc.gpsimd.tensor_tensor(out=tile_[:, cols], in0=h_rows[b][:, 1, cols], in1=h_rows[b][:, 0, cols], op=ALU.subtract)
+                gaps[(b, half)] = tile_[:, cols]
+
+        def base_tensor(b):
+            for half in range(HALVES):
+                cols = half_cols(half)
+                bank = psum_gap.tile([P, BANK], F32, tag="gap", name="base_bank")
+                nc.tensor.matmul(out=bank[:], lhsT=diagonal[1.0][:], rhs=h_rows[b][:, 0, cols], start=True, stop=False)
+                nc.tensor.matmul(out=bank[:], lhsT=diagonal[-1.0][:], rhs=h_rows[b][:, 2, cols], start=False, stop=True)
+                bases[(b, half)] = bank[:]
+
+        parts = {}
+
+        def blend_mul(b):
+            for half in range(HALVES):
+                cols = half_cols(half)
+                if half == 0:
+                    parts[b] = work.tile([P, H], F32, tag="part", name="part%d" % b)
+                nc.vector.tensor_tensor(out=parts[b][:, cols], in0=pair_term[b][:, cols], in1=gaps[(b, half)], op=ALU.mult)
+
+        def blend_add(b):
+            for half in range(HALVES):
+                cols = half_cols(half)
+                nc.vector.tensor_tensor(out=offset[b][:, cols], in0=parts[b][:, cols], in1=bases[(b, half)], op=ALU.add)
 
         def clamp(b, half):
             nc.scalar.activation(out=pair_lse[b][:, half_cols(half)], in_=score_banks[(b, 1, half)][:], func=ACT.Relu, bias=shift_up[:], scale=1.0)
@@ -326,16 +376,6 @@ def tile_blocksa_pa_kernel(tc, h, s2t_W1_w, s2t_W1_b, s2t_W_w, out):
                 clamp(b, half)
             for half in range(HALVES):
                 sigma(b, half)
-
-        def blend(b):
-            parts = []
-            for half in range(HALVES):
-                part = work.tile([P, BANK], F32, tag="part")
-                nc.vector.tensor_tensor(out=part[:], in0=pair_term[b][:, half_cols(half)], in1=gaps[(b, half)], op=ALU.mult)
-                parts.append(part)
-            for half in range(HALVES):
-                cols = half_cols(half)
-                nc.vector.tensor_tensor(out=offset[b][:, cols], in0=parts[half][:], in1=offset[b][:, cols], op=ALU.add)
 
         logs = {}
 
@@ -442,6 +482,11 @@ def tile_blocksa_pa_kernel(tc, h, s2t_W1_w, s2t_W1_b, s2t_W_w, out):
             logs[b] = work.tile([P, H], F32, tag="log", bufs=LOGBUFS, name="log%d" % b)
             nc.scalar.activation(out=logs[b][:], in_=pair_term[b][:], func=ACT.Ln)
 
+        def merge_gpsimd(b):
+            for half in range(HALVES):
+                cols = half_cols(half)
+                nc.gpsimd.tensor_tensor(out=pair_lse[b][:, cols], in0=pair_lse[b][:, cols], in1=logs[b][:, cols], op=ALU.subtract)
+
         def merge_wide(b):
             nc.vector.tensor_tensor(out=pair_lse[b][:], in0=pair_lse[b][:], in1=logs[b][:], op=ALU.subtract)
 
@@ -476,10 +521,10 @@ def tile_blocksa_pa_kernel(tc, h, s2t_W1_w, s2t_W1_b, s2t_W_w, out):
         quantise_tokens(1)
         hidden_matmuls(0)
         transpose_tokens(2)
+        base_vector(0)
         hidden_relus(0)
         hidden_copies(0,0)
         tok(2,"SV")
-
         w2_transposes(0)
         w2_copies(0,"SS")
         hidden_copies(0,1)
@@ -490,7 +535,6 @@ def tile_blocksa_pa_kernel(tc, h, s2t_W1_w, s2t_W1_b, s2t_W_w, out):
         w2_transposes(1)
         hidden_relus(1)
         w2_copies(1,"SS")
-        base(0)
         w2_transposes(2)
         w2_copies(2,"VS")
         w2_quantise(1)
@@ -502,86 +546,86 @@ def tile_blocksa_pa_kernel(tc, h, s2t_W1_w, s2t_W1_b, s2t_W_w, out):
         w2_transposes(3)
         hidden_relus(2)
         w2_copies(3,"VS")
-        base(1)
-        w2_quantise(3)
 
-        transpose_tokens(4)
-        tok(4,"SS")
         transpose_tokens(3)
+        w2_quantise(3)
         tok(3,"SS")
-        quantise_tokens(4)
+        transpose_tokens(4)
+        tok(4,"SV")
         quantise_tokens(3)
         hidden_copies(2,0)
         hidden_copies(2,1)
-        base(2)
-
         d1(0)
+        hidden_matmuls(3)
+        quantise_f(2)
+        quantise_tokens(4)
         first_clamp(0)
         first_sigma(0)
-        hidden_matmuls(4)
         d1(1)
-        quantise_f(2)
-        hidden_relus(4)
-        first_clamp(1)
-        blend(0)
-        gap_vector(1)
-        base(3)
-        transpose_tokens(5)
-        tok(5,"SS")
-        first_sigma(1)
-        hidden_copies(4,0)
-        hidden_copies(4,1)
-        quantise_tokens(5)
-        hidden_matmuls(3)
-        blend(1)
-        d1(2)
         hidden_relus(3)
-        first_clamp(2)
-        first_sigma(2)
-        gap(2)
+        blend_mul(0)
+        blend_add(0)
+        d1(2)
+        first_clamp(1)
+        first_sigma(1)
+        gap_vector(1)
+        base_vector(1)
         hidden_copies(3,0)
         hidden_copies(3,1)
+        hidden_matmuls(4)
         quantise_f(3)
-        quantise_f(4)
-        hidden_matmuls(5)
+        first_clamp(2)
+        hidden_relus(4)
+        first_sigma(2)
+        blend_mul(1)
+        blend_add(1)
         d1(3)
-        gap(3)
-        hidden_relus(5)
-        blend(2)
+        gap(2)
+        transpose_tokens(5)
+        hidden_copies(4,0)
+        hidden_copies(4,1)
+        quantise_f(4)
         first_clamp(3)
         first_sigma(3)
+        base_vector(2)
+        tok(5,"SV")
+        blend_mul(2)
+        quantise_tokens(5)
+        d2(0)
+        gap(3)
+        blend_add(2)
+        log_wide(0)
+        merge_gpsimd(0)
+        hidden_matmuls(5)
+        log_wide(1)
+        merge_gpsimd(1)
+        hidden_relus(5)
+        blend_mul(3)
+        lead(0)
+        base_tensor(3)
+        d2(1)
+        log_wide(2)
+        merge_gpsimd(2)
+        log_wide(3)
+        merge_gpsimd(3)
         hidden_copies(5,0)
         hidden_copies(5,1)
-        d2(0)
         quantise_f(5)
-
-        log_wide(0)
-        log_wide(1)
-        blend(3)
-        log_wide(2)
-        log_wide(3)
-        merge_wide(0)
-        merge_wide(1)
-        lead(0)
-        d2(1)
-        d2(2)
-        d2(3)
-        merge_wide(2)
         lead(1)
         last_sigma(0)
+        blend_add(3)
         last_sigma(1)
+        d2(2)
         weigh(0)
-        merge_wide(3)
+        d2(3)
         lead(2)
+        weigh(1)
         last_sigma(2)
         sum_tensor(0)
-        weigh(1)
         lead(3)
-        sum_tensor(1)
         store_sum(0)
         last_sigma(3)
-        weigh(2)
+        finish(2)
+        sum_tensor(1)
         store_sum(1)
-        sum_tensor(2)
         finish(3)
-        store_sum(2)

@@ -251,6 +251,17 @@ def tile_blocksa_pa_kernel(tc, h, s2t_W1_w, s2t_W1_b, s2t_W_w, out):
                     scale=1.0,
                 )
 
+        def hidden_relus_vector(s, tiles):
+            for m in [m + 1 - 2 * (m % 2) for m in tiles]:
+                nc.vector.tensor_scalar(
+                    out=f_rows_of[s][:, m, :],
+                    in0=f_banks[(s, m // 2)][:, m % 2, :],
+                    scalar1=bias[:, m : m + 1],
+                    scalar2=0.0,
+                    op0=ALU.add,
+                    op1=ALU.max,
+                )
+
         def hidden_rows(s):
             hidden_matmuls(s)
             hidden_relus(s)
@@ -262,6 +273,17 @@ def tile_blocksa_pa_kernel(tc, h, s2t_W1_w, s2t_W1_b, s2t_W_w, out):
                 cols = slice(0, PIECE) if side is None else slice(side * P, (side + 1) * P)
                 grouped_side = f_grouped_of[s][:, g, cols, :].rearrange("q (c i) t -> q c t i", i=RUN)
                 rows_side = f_rows_of[s][:, g * PACK : (g + 1) * PACK, cols].rearrange("q t (c i) -> q c t i", i=RUN)
+                if (s, side) in token_0_sides:
+                    nc.vector.tensor_scalar_mul(out=grouped_side, in0=rows_side, scalar1=-1.0)
+                else:
+                    nc.vector.tensor_copy(out=grouped_side, in_=rows_side)
+
+        def hidden_copies_whole(s):
+            f_grouped_of[s] = hidden.tile([P, PASSES, PIECE, PACK], BF16, tag="f_grouped", align_bytes=64, name="f_grouped%d" % s)
+            for side in range(SIDES) if s < BATCHES else [None]:
+                cols = slice(0, PIECE) if side is None else slice(side * P, (side + 1) * P)
+                grouped_side = f_grouped_of[s][:, :, cols, :].rearrange("q g (c i) t -> q g c t i", i=RUN)
+                rows_side = f_rows_of[s][:].rearrange("q (g t) n -> q g t n", t=PACK)[:, :, :, cols].rearrange("q g t (c i) -> q g c t i", i=RUN)
                 if (s, side) in token_0_sides:
                     nc.vector.tensor_scalar_mul(out=grouped_side, in0=rows_side, scalar1=-1.0)
                 else:
@@ -329,7 +351,7 @@ def tile_blocksa_pa_kernel(tc, h, s2t_W1_w, s2t_W1_b, s2t_W_w, out):
                     nc.vector.tensor_tensor(out=bases[(b, half)], in0=h_rows[b][:, 0, cols], in1=h_rows[b][:, 2, cols], op=ALU.subtract)
 
         def base_gpsimd(b):
-            tile_ = work.tile([P, H], F32, tag="baseg", bufs=GBUFS, name="baseg%d" % b)
+            tile_ = offset[b]
             for half in range(HALVES):
                 cols = half_cols(half)
                 nc.gpsimd.tensor_tensor(out=tile_[:, cols], in0=h_rows[b][:, 0, cols], in1=h_rows[b][:, 2, cols], op=ALU.subtract)
@@ -546,7 +568,6 @@ def tile_blocksa_pa_kernel(tc, h, s2t_W1_w, s2t_W1_b, s2t_W_w, out):
         w2_transposes(3)
         hidden_relus(2)
         w2_copies(3,"VS")
-
         transpose_tokens(3)
         w2_quantise(3)
         tok(3,"SS")
@@ -555,6 +576,8 @@ def tile_blocksa_pa_kernel(tc, h, s2t_W1_w, s2t_W1_b, s2t_W_w, out):
         quantise_tokens(3)
         hidden_copies(2,0)
         hidden_copies(2,1)
+        base_gpsimd(1)
+        base_gpsimd(2)
         d1(0)
         hidden_matmuls(3)
         quantise_f(2)
@@ -569,26 +592,25 @@ def tile_blocksa_pa_kernel(tc, h, s2t_W1_w, s2t_W1_b, s2t_W_w, out):
         first_clamp(1)
         first_sigma(1)
         gap_vector(1)
-        base_vector(1)
         hidden_copies(3,0)
         hidden_copies(3,1)
         hidden_matmuls(4)
         quantise_f(3)
         first_clamp(2)
-        hidden_relus(4)
+        hidden_relus(4, range(0, 6))
         first_sigma(2)
         blend_mul(1)
         blend_add(1)
         d1(3)
         gap(2)
         transpose_tokens(5)
+        hidden_relus_vector(4, range(6, 8))
         hidden_copies(4,0)
         hidden_copies(4,1)
         quantise_f(4)
         first_clamp(3)
         first_sigma(3)
-        base_vector(2)
-        tok(5,"SV")
+        tok(5,"VV")
         blend_mul(2)
         quantise_tokens(5)
         d2(0)

from contextlib import ExitStack

import concourse.mybir as mybir
from concourse.masks import make_identity

F32 = mybir.dt.float32
BF16 = mybir.dt.bfloat16
U32 = mybir.dt.uint32
U8 = mybir.dt.uint8
FP8X4 = mybir.dt.float8_e4m3fn_x4
ACT = mybir.ActivationFunctionType
ALU = mybir.AluOpType

P = 128
BATCHES = 4
TOKENS = 3
H = 1024
PACK = 4
PASSES = H // (P * PACK)
PLANES = 2
SIDES = 2
PIECE = SIDES * P
WEIGHT_PIECES = H // PIECE
TOKEN_PIECES = BATCHES * TOKENS * P // PIECE
ROW_TILES = H // P
BANK = 512
SHIFT = 16.0
LOGBUFS = 4
GBUFS = 1
WARM = 6
HALVES = H // BANK
RUN = 4

FLOPS = 2 * 2 * BATCHES * P * TOKENS * H * H


def tile_blocksa_pa_kernel(tc, h, s2t_W1_w, s2t_W1_b, s2t_W_w, out):
    nc = tc.nc
    h_flat = h.rearrange("b n j k -> (b n) (j k)")
    out_flat = out.rearrange("b n c -> (b n) c")

    with ExitStack() as stack:
        consts = stack.enter_context(tc.tile_pool(name="consts", bufs=1))
        keep = stack.enter_context(tc.tile_pool(name="keep", bufs=1))
        raw = stack.enter_context(tc.tile_pool(name="raw", bufs=8))
        stage = stack.enter_context(tc.tile_pool(name="stage", bufs=4))
        hidden = stack.enter_context(tc.tile_pool(name="hidden", bufs=3))
        work = stack.enter_context(tc.tile_pool(name="work", bufs=2))
        psum = stack.enter_context(tc.psum_pool(name="psum", bufs=6))
        psum_gap = stack.enter_context(tc.psum_pool(name="psum_gap", bufs=2))
        stack.enter_context(tc.manual_schedule())

        bias_rows = consts.tile([P, 2 * P], BF16)
        nc.vector.memset(bias_rows[:], 0.0)
        bias = consts.tile([P, ROW_TILES], F32)
        shift_up = consts.tile([P, 1], F32)
        nc.vector.memset(shift_up[:], SHIFT)
        shift_down = consts.tile([P, 1], F32)
        nc.vector.memset(shift_down[:], -SHIFT)

        ident = consts.tile([P, P], F32)
        make_identity(nc, ident[:])
        diagonal = {}
        for value in (1.0, -1.0):
            scaled = consts.tile([P, P], BF16, name="diagonal%d" % len(diagonal))
            nc.vector.tensor_scalar_mul(out=scaled[:], in0=ident[:], scalar1=value)
            diagonal[value] = scaled

        def spread_bias():
            bias_bank = psum.tile([P, BANK], F32, tag="bank")
            nc.tensor.transpose(bias_bank[:, 0:P], bias_rows[:].bitcast(F32), ident[:])
            bias_pairs = consts.tile([P, WEIGHT_PIECES], F32)
            nc.vector.tensor_copy(out=bias_pairs[:], in_=bias_bank[:, 0:WEIGHT_PIECES])
            nc.vector.tensor_copy(out=bias[:], in_=bias_pairs[:].bitcast(BF16))

        zeros = consts.tile([P, BANK], BF16)
        nc.vector.memset(zeros[:], 0.0)
        warm_bank = psum_gap.tile([P, BANK], F32, tag="gap", name="warm_bank")
        for i in range(WARM):
            nc.tensor.matmul(out=warm_bank[:], lhsT=zeros[:, 0:P], rhs=zeros[:], start=True, stop=True)
        warm = consts.tile([P, 1], F32)
        nc.scalar.activation(out=warm[:], in_=shift_up[:], func=ACT.Sigmoid)

        h_rows = []
        for b in range(BATCHES):
            h_rows.append(keep.tile([P, TOKENS, H], BF16, name="h_rows%d" % b))

        def load_tokens(b, j_from, j_to):
            nc.sync.dma_start(
                out=h_rows[b][:, j_from:j_to, :].rearrange("n j k -> n (j k)"),
                in_=h_flat[b * P : (b + 1) * P, j_from * H : j_to * H],
            )

        load_tokens(0, 0, SIDES)

        w1_raw = []
        for r in range(WEIGHT_PIECES):
            rows = raw.tile([P, SIDES, H], BF16, tag="raw", name="w1_raw%d" % r)
            nc.sync.dma_start(
                out=rows[:].rearrange("q e k -> q (e k)"),
                in_=s2t_W1_w[r * PIECE : (r + 1) * PIECE, :].rearrange("(q e) k -> q (e k)", e=SIDES),
            )
            w1_raw.append(rows)
        nc.sync.dma_start(
            out=bias_rows[0:WEIGHT_PIECES, :],
            in_=s2t_W1_b.rearrange("(r c) -> r c", r=WEIGHT_PIECES),
        )
        load_tokens(1, 0, SIDES)
        load_tokens(0, SIDES, TOKENS)
        load_tokens(2, 0, SIDES)

        w2_raw = []
        for r in range(WEIGHT_PIECES):
            rows = raw.tile([P, SIDES, H], BF16, tag="raw", name="w2_raw%d" % r)
            nc.sync.dma_start(
                out=rows[:],
                in_=s2t_W_w[r * PIECE : (r + 1) * PIECE, :].rearrange("(i q) k -> q i k", q=P),
            )
            w2_raw.append(rows)

        load_tokens(3, 0, SIDES)
        load_tokens(1, SIDES, TOKENS)
        for b in range(SIDES, BATCHES):
            load_tokens(b, SIDES, TOKENS)

        w1_codes = keep.tile([P, WEIGHT_PIECES, PASSES, PIECE], U32, align_bytes=64)
        w1_scales = keep.tile([P, WEIGHT_PIECES, PASSES, PIECE], U8, align_bytes=64)
        w2_codes = keep.tile([P, PASSES, H], U32, align_bytes=64)
        w2_scales = keep.tile([P, PASSES, H], U8, align_bytes=64)
        f_codes = []
        f_scales = []
        for s in range(TOKEN_PIECES):
            f_codes.append(keep.tile([P, PASSES, PIECE], U32, align_bytes=64, name="f_codes%d" % s))
            f_scales.append(keep.tile([P, PASSES, PIECE], U8, align_bytes=64, name="f_scales%d" % s))

        pair_lse = []
        pair_term = []
        offset = []
        for b in range(BATCHES):
            pair_lse.append(keep.tile([P, H], F32, name="pair_lse%d" % b))
            pair_term.append(keep.tile([P, H], F32, name="pair_term%d" % b))
            offset.append(keep.tile([P, H], F32, name="offset%d" % b))

        def token_rows(s):
            if s < BATCHES:
                return [h_rows[s][:, 0, :], h_rows[s][:, 1, :]]
            batch = SIDES * (s - BATCHES)
            return [h_rows[batch][:, 2, :], h_rows[batch + 1][:, 2, :]]

        def piece_of(b, j):
            if j < SIDES:
                return b, j
            return BATCHES + b // SIDES, b % SIDES

        token_0_sides = [piece_of(b, 0) for b in range(BATCHES)]

        def transpose_piece(row_tiles):
            banks = []
            for side in range(SIDES):
                words = row_tiles[side].bitcast(F32)
                bank = psum.tile([P, PASSES, PLANES, P], F32, tag="bank")
                for g in range(PASSES):
                    for u in range(PLANES):
                        start = (g * PLANES + u) * P
                        nc.tensor.transpose(bank[:, g, u, :], words[:, start : start + P], ident[:])
                banks.append(bank)
            return banks

        def copy_piece(banks, copies):
            grouped = stage.tile([P, PASSES, PIECE, PACK], BF16, tag="grouped", align_bytes=64)
            grouped_words = (
                grouped[:]
                .rearrange("q g c t -> q (g c t)")
                .bitcast(F32)
                .rearrange("q (g c u) -> q g c u", g=PASSES, u=PLANES)
            )
            for side in range(SIDES):
                copies[side](
                    out=grouped_words[:, :, side * P : (side + 1) * P, :],
                    in_=banks[side][:].rearrange("q g u c -> q g c u"),
                )
            return grouped

        def quantise_whole(grouped, codes, scales):
            nc.vector.quantize_mx(
                out=codes.rearrange("q g c -> q (g c)").bitcast(FP8X4),
                scales=scales.rearrange("q g c -> q (g c)"),
                in_=grouped[:].rearrange("q g c t -> q (g c t)"),
            )

        def quantise_piece(grouped, codes, scales):
            for g in range(PASSES):
                nc.vector.quantize_mx(
                    out=codes[:, g, :].bitcast(FP8X4),
                    scales=scales[:, g, :],
                    in_=grouped[:, g, :, :].rearrange("q c t -> q (c t)"),
                )

        both_engines = [nc.scalar.copy, nc.vector.tensor_copy]
        scalar_only = [nc.scalar.copy, nc.scalar.copy]
        vector_only = [nc.vector.tensor_copy, nc.vector.tensor_copy]

        token_banks = {}
        token_grouped = {}
        token_codes = {}
        token_scales = {}

        def transpose_tokens(s):
            token_banks[s] = transpose_piece(token_rows(s))

        def copy_tokens(s, copies):
            token_grouped[s] = copy_piece(token_banks[s], copies)

        def quantise_tokens(s):
            codes = stage.tile([P, PASSES, PIECE], U32, tag="token_codes", align_bytes=64)
            scales = stage.tile([P, PASSES, PIECE], U8, tag="token_scales", align_bytes=64)
            quantise_whole(token_grouped[s], codes[:], scales[:])
            token_codes[s] = codes
            token_scales[s] = scales

        f_rows_of = {}
        f_banks = {}
        f_grouped_of = {}

        def hidden_matmuls(s, tiles=range(ROW_TILES)):
            for m in tiles:
                if m % 2 == 0:
                    bank = psum.tile([P, 2, PIECE], F32, tag="bank", name="f_bank")
                    f_banks[(s, m // 2)] = bank
                bank = f_banks[(s, m // 2)]
                for g in range(PASSES):
                    nc.tensor.matmul_mx(
                        out=bank[:, m % 2, :],
                        lhsT=w1_codes[:, m // 2, g, (m % 2) * P : (m % 2 + 1) * P].bitcast(FP8X4),
                        lhsT_scale=w1_scales[:, m // 2, g, (m % 2) * P : (m % 2 + 1) * P],
                        rhs=token_codes[s][:, g, :].bitcast(FP8X4),
                        rhs_scale=token_scales[s][:, g, :],
                        start=(g == 0),
                        stop=(g == PASSES - 1),
                    )

        def hidden_relus(s, tiles=range(ROW_TILES)):
            if s not in f_rows_of:
                f_rows_of[s] = hidden.tile([P, ROW_TILES, PIECE], BF16, tag="f_rows", name="f_rows%d" % s)
            for m in [m + 1 - 2 * (m % 2) for m in tiles]:
                nc.scalar.activation(
                    out=f_rows_of[s][:, m, :],
                    in_=f_banks[(s, m // 2)][:, m % 2, :],
                    func=ACT.Relu,
                    bias=bias[:, m : m + 1],
                    scale=1.0,
                )

        def hidden_relus_vector(s, tiles):
            for m in [m + 1 - 2 * (m % 2) for m in tiles]:
                nc.vector.tensor_scalar(
                    out=f_rows_of[s][:, m, :],
                    in0=f_banks[(s, m // 2)][:, m % 2, :],
                    scalar1=bias[:, m : m + 1],
                    scalar2=0.0,
                    op0=ALU.add,
                    op1=ALU.max,
                )

        def hidden_rows(s):
            hidden_matmuls(s)
            hidden_relus(s)

        def hidden_copies(s, g):
            if s not in f_grouped_of:
                f_grouped_of[s] = hidden.tile([P, PASSES, PIECE, PACK], BF16, tag="f_grouped", align_bytes=64, name="f_grouped%d" % s)
            for side in range(SIDES) if s < BATCHES else [None]:
                cols = slice(0, PIECE) if side is None else slice(side * P, (side + 1) * P)
                grouped_side = f_grouped_of[s][:, g, cols, :].rearrange("q (c i) t -> q c t i", i=RUN)
                rows_side = f_rows_of[s][:, g * PACK : (g + 1) * PACK, cols].rearrange("q t (c i) -> q c t i", i=RUN)
                if (s, side) in token_0_sides:
                    nc.vector.tensor_scalar_mul(out=grouped_side, in0=rows_side, scalar1=-1.0)
                else:
                    nc.vector.tensor_copy(out=grouped_side, in_=rows_side)

        def hidden_copies_whole(s):
            f_grouped_of[s] = hidden.tile([P, PASSES, PIECE, PACK], BF16, tag="f_grouped", align_bytes=64, name="f_grouped%d" % s)
            for side in range(SIDES) if s < BATCHES else [None]:
                cols = slice(0, PIECE) if side is None else slice(side * P, (side + 1) * P)
                grouped_side = f_grouped_of[s][:, :, cols, :].rearrange("q g (c i) t -> q g c t i", i=RUN)
                rows_side = f_rows_of[s][:].rearrange("q (g t) n -> q g t n", t=PACK)[:, :, :, cols].rearrange("q g t (c i) -> q g c t i", i=RUN)
                if (s, side) in token_0_sides:
                    nc.vector.tensor_scalar_mul(out=grouped_side, in0=rows_side, scalar1=-1.0)
                else:
                    nc.vector.tensor_copy(out=grouped_side, in_=rows_side)

        def hidden_codes(s):
            for g in range(PASSES):
                hidden_copies(s, g)
            quantise_f(s)

        def quantise_f(s):
            quantise_whole(f_grouped_of[s], f_codes[s][:], f_scales[s][:])

        score_banks = {}

        def scores(b, j, half):
            bank = psum.tile([P, BANK], F32, tag="bank")
            score_banks[(b, j, half)] = bank
            for token in (j, 0):
                s, side = piece_of(b, token)
                for g in range(PASSES):
                    nc.tensor.matmul_mx(
                        out=bank[:],
                        lhsT=f_codes[s][:, g, side * P : (side + 1) * P].bitcast(FP8X4),
                        lhsT_scale=f_scales[s][:, g, side * P : (side + 1) * P],
                        rhs=w2_codes[:, g, half * BANK : (half + 1) * BANK].bitcast(FP8X4),
                        rhs_scale=w2_scales[:, g, half * BANK : (half + 1) * BANK],
                        start=(token == j and g == 0),
                        stop=(token == 0 and g == PASSES - 1),
                    )

        def half_cols(half):
            return slice(half * BANK, (half + 1) * BANK)

        gaps = {}
        bases = {}

        def gap(b, halves=range(HALVES)):
            for half in halves:
                cols = half_cols(half)
                bank = psum_gap.tile([P, BANK], F32, tag="gap")
                nc.tensor.matmul(out=bank[:], lhsT=diagonal[1.0][:], rhs=h_rows[b][:, 1, cols], start=True, stop=False)
                nc.tensor.matmul(out=bank[:], lhsT=diagonal[-1.0][:], rhs=h_rows[b][:, 0, cols], start=False, stop=True)
                gaps[(b, half)] = bank[:]

        def gap_term(b, half, token):
            cols = half_cols(half)
            if token == 1:
                gaps[(b, half)] = psum_gap.tile([P, BANK], F32, tag="gap", name="gap_bank")[:]
            nc.tensor.matmul(out=gaps[(b, half)], lhsT=diagonal[1.0 if token == 1 else -1.0][:], rhs=h_rows[b][:, token, cols], start=(token == 1), stop=(token == 0))

        def gap_vector(b):
            tile_ = work.tile([P, H], F32, tag="gapv", bufs=1, name="gapv%d" % b)
            nc.vector.tensor_tensor(out=tile_[:], in0=h_rows[b][:, 1, :], in1=h_rows[b][:, 0, :], op=ALU.subtract)
            for half in range(HALVES):
                gaps[(b, half)] = tile_[:, half_cols(half)]

        def base_vector(b, halves=range(HALVES)):
            if len(halves) == HALVES:
                nc.vector.tensor_tensor(out=offset[b][:], in0=h_rows[b][:, 0, :], in1=h_rows[b][:, 2, :], op=ALU.subtract)
            for half in halves:
                cols = half_cols(half)
                bases[(b, half)] = offset[b][:, cols]
                if len(halves) < HALVES:
                    nc.vector.tensor_tensor(out=bases[(b, half)], in0=h_rows[b][:, 0, cols], in1=h_rows[b][:, 2, cols], op=ALU.subtract)

        def base_gpsimd(b):
            tile_ = offset[b]
            for half in range(HALVES):
                cols = half_cols(half)
                nc.gpsimd.tensor_tensor(out=tile_[:, cols], in0=h_rows[b][:, 0, cols], in1=h_rows[b][:, 2, cols], op=ALU.subtract)
                bases[(b, half)] = tile_[:, cols]

        def gap_gpsimd(b):
            tile_ = work.tile([P, H], F32, tag="gapg", bufs=GBUFS, name="gapg%d" % b)
            for half in range(HALVES):
                cols = half_cols(half)
                nc.gpsimd.tensor_tensor(out=tile_[:, cols], in0=h_rows[b][:, 1, cols], in1=h_rows[b][:, 0, cols], op=ALU.subtract)
                gaps[(b, half)] = tile_[:, cols]

        def base_tensor(b):
            for half in range(HALVES):
                cols = half_cols(half)
                bank = psum_gap.tile([P, BANK], F32, tag="gap", name="base_bank")
                nc.tensor.matmul(out=bank[:], lhsT=diagonal[1.0][:], rhs=h_rows[b][:, 0, cols], start=True, stop=False)
                nc.tensor.matmul(out=bank[:], lhsT=diagonal[-1.0][:], rhs=h_rows[b][:, 2, cols], start=False, stop=True)
                bases[(b, half)] = bank[:]

        parts = {}

        def blend_mul(b):
            for half in range(HALVES):
                cols = half_cols(half)
                if half == 0:
                    parts[b] = work.tile([P, H], F32, tag="part", name="part%d" % b)
                nc.vector.tensor_tensor(out=parts[b][:, cols], in0=pair_term[b][:, cols], in1=gaps[(b, half)], op=ALU.mult)

        def blend_add(b):
            for half in range(HALVES):
                cols = half_cols(half)
                nc.vector.tensor_tensor(out=offset[b][:, cols], in0=parts[b][:, cols], in1=bases[(b, half)], op=ALU.add)

        def clamp(b, half):
            nc.scalar.activation(out=pair_lse[b][:, half_cols(half)], in_=score_banks[(b, 1, half)][:], func=ACT.Relu, bias=shift_up[:], scale=1.0)

        def sigma(b, half):
            cols = half_cols(half)
            nc.scalar.activation(out=pair_term[b][:, cols], in_=pair_lse[b][:, cols], func=ACT.Sigmoid, bias=shift_down[:], scale=1.0)

        def first_functions(b):
            for half in range(HALVES):
                clamp(b, half)
            for half in range(HALVES):
                sigma(b, half)

        logs = {}

        def logarithm(b):
            logs[b] = work.tile([P, H], F32, tag="log", bufs=LOGBUFS, name="log%d" % b)
            for half in range(HALVES):
                cols = half_cols(half)
                nc.scalar.activation(out=logs[b][:, cols], in_=pair_term[b][:, cols], func=ACT.Ln)

        def merge(b):
            for half in range(HALVES):
                cols = half_cols(half)
                nc.vector.tensor_tensor(out=pair_lse[b][:, cols], in0=pair_lse[b][:, cols], in1=logs[b][:, cols], op=ALU.subtract)

        def lead(b):
            for half in range(HALVES):
                cols = half_cols(half)
                nc.vector.tensor_tensor(out=pair_lse[b][:, cols], in0=pair_lse[b][:, cols], in1=score_banks[(b, 2, half)][:], op=ALU.subtract)

        def last_sigma(b):
            for half in range(HALVES):
                cols = half_cols(half)
                nc.scalar.activation(out=pair_lse[b][:, cols], in_=pair_lse[b][:, cols], func=ACT.Sigmoid, bias=shift_down[:], scale=1.0)

        def finish(b):
            for half in range(HALVES):
                cols = half_cols(half)
                nc.vector.tensor_tensor(out=offset[b][:, cols], in0=offset[b][:, cols], in1=pair_lse[b][:, cols], op=ALU.mult)
            for half in range(HALVES):
                cols = half_cols(half)
                nc.vector.tensor_tensor(out=offset[b][:, cols], in0=offset[b][:, cols], in1=h_rows[b][:, 2, cols], op=ALU.add)
                nc.sync.dma_start(out=out_flat[b * P : (b + 1) * P, cols], in_=offset[b][:, cols])

        sum_banks = {}

        def weigh(b):
            for half in range(HALVES):
                cols = half_cols(half)
                nc.vector.tensor_tensor(out=offset[b][:, cols], in0=offset[b][:, cols], in1=pair_lse[b][:, cols], op=ALU.mult)

        def sum_tensor(b):
            for half in range(HALVES):
                cols = half_cols(half)
                bank = psum.tile([P, BANK], F32, tag="bank", name="sum_bank")
                nc.tensor.matmul(out=bank[:], lhsT=diagonal[1.0][:], rhs=h_rows[b][:, 2, cols], start=True, stop=False)
                nc.tensor.matmul(out=bank[:], lhsT=ident[:], rhs=offset[b][:, cols], start=False, stop=True)
                sum_banks[(b, half)] = bank

        def store_sum(b):
            for half in range(HALVES):
                cols = half_cols(half)
                nc.scalar.copy(out=pair_term[b][:, cols], in_=sum_banks[(b, half)][:])
                nc.sync.dma_start(out=out_flat[b * P : (b + 1) * P, cols], in_=pair_term[b][:, cols])

        def d1(b):
            for half in range(HALVES):
                scores(b, 1, half)

        def d2(b):
            for half in range(HALVES):
                scores(b, 2, half)

        copiers = {"S": nc.scalar.copy, "V": nc.vector.tensor_copy}

        def tok(s, who):
            copy_tokens(s, [copiers[who[0]], copiers[who[1]]])

        def w1(r, who):
            prepare_weights(w1_raw, w1_codes, w1_scales, r, [copiers[who[0]], copiers[who[1]]])

        w2_banks = {}
        w2_grouped = {}

        def w2_transposes(r):
            w2_banks[r] = transpose_piece([w2_raw[r][:, 0, :], w2_raw[r][:, 1, :]])

        def w2_copies(r, who):
            w2_grouped[r] = copy_piece(w2_banks[r], [copiers[who[0]], copiers[who[1]]])

        def w2_quantise(r):
            cols = slice(r * PIECE, (r + 1) * PIECE)
            quantise_piece(w2_grouped[r], w2_codes[:, :, cols], w2_scales[:, :, cols])

        w1_banks = {}
        w1_grouped = {}

        def w1_transposes(r):
            w1_banks[r] = transpose_piece([w1_raw[r][:, 0, :], w1_raw[r][:, 1, :]])

        def w1_copies(r, who):
            w1_grouped[r] = copy_piece(w1_banks[r], [copiers[who[0]], copiers[who[1]]])

        def w1_quantise(r):
            quantise_whole(w1_grouped[r], w1_codes[:, r], w1_scales[:, r])

        def first_clamp(b):
            for half in range(HALVES):
                clamp(b, half)

        def first_sigma(b):
            nc.scalar.activation(out=pair_term[b][:], in_=pair_lse[b][:], func=ACT.Sigmoid, bias=shift_down[:], scale=1.0)

        def log_wide(b):
            logs[b] = work.tile([P, H], F32, tag="log", bufs=LOGBUFS, name="log%d" % b)
            nc.scalar.activation(out=logs[b][:], in_=pair_term[b][:], func=ACT.Ln)

        def merge_gpsimd(b):
            for half in range(HALVES):
                cols = half_cols(half)
                nc.gpsimd.tensor_tensor(out=pair_lse[b][:, cols], in0=pair_lse[b][:, cols], in1=logs[b][:, cols], op=ALU.subtract)

        def merge_wide(b):
            nc.vector.tensor_tensor(out=pair_lse[b][:], in0=pair_lse[b][:], in1=logs[b][:], op=ALU.subtract)

        def prepare_weights(raw_pieces, codes, scales, r, copies):
            grouped = copy_piece(transpose_piece([raw_pieces[r][:, 0, :], raw_pieces[r][:, 1, :]]), copies)
            if codes is w1_codes:
                quantise_whole(grouped, codes[:, r], scales[:, r])
            else:
                cols = slice(r * PIECE, (r + 1) * PIECE)
                quantise_piece(grouped, codes[:, :, cols], scales[:, :, cols])

        transpose_tokens(0)
        tok(0,"SV")
        w1_transposes(0)
        gap(0,[0])
        w1_copies(0,"VS")
        quantise_tokens(0)
        w1_transposes(1)
        w1_copies(1,"VS")
        w1_transposes(2)
        gap(0,[1])
        w1_quantise(0)
        w1_copies(2,"SS")
        w1_quantise(1)
        w1_transposes(3)
        spread_bias()
        w1_copies(3,"VS")
        w1_quantise(2)
        transpose_tokens(1)
        w1_quantise(3)
        tok(1,"SV")
        quantise_tokens(1)
        hidden_matmuls(0)
        transpose_tokens(2)
        base_vector(0)
        hidden_relus(0)
        hidden_copies(0,0)
        tok(2,"SV")
        w2_transposes(0)
        w2_copies(0,"SS")
        hidden_copies(0,1)
        quantise_tokens(2)
        hidden_matmuls(1)
        quantise_f(0)
        w2_quantise(0)
        w2_transposes(1)
        hidden_relus(1)
        w2_copies(1,"SS")
        w2_transposes(2)
        w2_copies(2,"VS")
        w2_quantise(1)
        hidden_copies(1,0)
        hidden_copies(1,1)
        w2_quantise(2)
        quantise_f(1)
        hidden_matmuls(2)
        w2_transposes(3)
        hidden_relus(2)
        w2_copies(3,"VS")
        transpose_tokens(3)
        w2_quantise(3)
        tok(3,"SS")
        transpose_tokens(4)
        tok(4,"SV")
        quantise_tokens(3)
        hidden_copies(2,0)
        hidden_copies(2,1)
        base_gpsimd(1)
        base_gpsimd(2)
        d1(0)
        hidden_matmuls(3)
        quantise_f(2)
        quantise_tokens(4)
        first_clamp(0)
        first_sigma(0)
        d1(1)
        hidden_relus(3)
        blend_mul(0)
        blend_add(0)
        d1(2)
        first_clamp(1)
        first_sigma(1)
        gap_vector(1)
        hidden_copies(3,0)
        hidden_copies(3,1)
        hidden_matmuls(4)
        quantise_f(3)
        first_clamp(2)
        hidden_relus(4, range(0, 6))
        first_sigma(2)
        blend_mul(1)
        blend_add(1)
        d1(3)
        gap(2)
        transpose_tokens(5)
        hidden_relus_vector(4, range(6, 8))
        hidden_copies(4,0)
        hidden_copies(4,1)
        quantise_f(4)
        first_clamp(3)
        first_sigma(3)
        tok(5,"VV")
        blend_mul(2)
        quantise_tokens(5)
        d2(0)
        gap(3)
        blend_add(2)
        log_wide(0)
        merge_gpsimd(0)
        hidden_matmuls(5)
        log_wide(1)
        merge_gpsimd(1)
        hidden_relus(5)
        blend_mul(3)
        lead(0)
        base_tensor(3)
        d2(1)
        log_wide(2)
        merge_gpsimd(2)
        log_wide(3)
        merge_gpsimd(3)
        hidden_copies(5,0)
        hidden_copies(5,1)
        quantise_f(5)
        lead(1)
        last_sigma(0)
        blend_add(3)
        last_sigma(1)
        d2(2)
        weigh(0)
        d2(3)
        lead(2)
        weigh(1)
        last_sigma(2)
        sum_tensor(0)
        lead(3)
        store_sum(0)
        last_sigma(3)
        finish(2)
        sum_tensor(1)
        store_sum(1)
        finish(3)
